import numpy as np
import ml_dtypes


def mxq(x, axis, fmt="e4m3"):
    dtype, down = {"e4m3": (ml_dtypes.float8_e4m3fn, 7), "e5m2": (ml_dtypes.float8_e5m2, 14)}[fmt]
    v = np.moveaxis(np.asarray(x, np.float32).astype(ml_dtypes.bfloat16).astype(np.float64), axis, -1)
    blocks = v.reshape(v.shape[:-1] + (-1, 32))
    amax = np.abs(blocks).max(-1, keepdims=True)
    byte = np.maximum(np.where(amax > 0, np.frexp(amax)[1] - 1 + 127, 0) - down, 1)
    scale = np.exp2(byte - 127.0)
    codes = (blocks / scale).astype(np.float32).astype(dtype).astype(np.float64)
    return np.moveaxis((codes * scale).reshape(v.shape), -1, axis)


WIDE = False


def mx_kscale(k):
    if not WIDE:
        return np.ones(k)
    levels = np.array([10, -10, 5, -5, 0])
    if k % 512:
        return np.exp2(np.random.permutation(np.resize(levels, k // 32))).repeat(32)
    a = np.empty((k // 512, 16))
    for p in range(k // 512):
        a[p, :8] = np.random.permutation(np.resize(levels, 8))
        for g in range(8):
            far = levels[np.abs(levels - a[p, g]) >= 10]
            a[p, g + 8] = far[np.random.randint(len(far))]
    return np.exp2(a.ravel()).repeat(32)


BF16 = ml_dtypes.bfloat16


def bf(x):
    return np.asarray(x, np.float32).astype(BF16)


def f64(x):
    return np.asarray(x).astype(np.float64)


B, DIN, H1, H2, N, I, K, O = 512, 2048, 1024, 512, 32, 16, 256, 16
NI = N * I
KO = K * O
SQ_EPS = 1e-8
G_SCALE = 64.0


def squash(t):
    sq = np.sum(t * t, axis=-1, keepdims=True)
    return (sq / (1.0 + sq)) * t / np.sqrt(sq + SQ_EPS)


def presquash(p, Wr):
    pf = f64(p).reshape(B, NI)
    wf = f64(Wr).transpose(0, 3, 1, 2).reshape(NI, KO)
    return (pf @ wf).reshape(B, K, O) * (1.0 / K)


def setup_inputs():
    v = mx_kscale(B)[:, None, None]
    u = mx_kscale(KO).reshape(K, O)[:, :1]
    p0 = bf(np.random.standard_normal((B, N, I)))
    Wr0 = bf(np.random.standard_normal((N, K, O, I)) * K / np.sqrt(NI * O))
    g = bf(np.random.standard_normal((B, K, O)) * np.exp2(np.random.randint(-6, 1, (B, 1, 1))) * G_SCALE / v * u)
    s = presquash(p0, Wr0)
    return {"p": bf(f64(p0) * v),
            "Wr": bf(f64(Wr0) / u[None, :, :, None]),
            "s": np.asarray(s, np.float32),
            "grad_out": g}


def reference(p, Wr, s, grad_out):
    c = 1.0 / K
    t = f64(s)
    g = f64(grad_out)
    q = np.sum(t * t, axis=-1, keepdims=True)
    r = 1.0 / np.sqrt(q + SQ_EPS)
    h = q / (1.0 + q) * r
    dh = r / (1.0 + q) ** 2 - 0.5 * q / (1.0 + q) * r ** 3
    dot = np.sum(t * g, axis=-1, keepdims=True)
    ds = h * g + 2.0 * dh * dot * t
    dsa = ds.reshape(B, KO)
    pf = f64(p).reshape(B, NI)
    wf = f64(Wr).transpose(0, 3, 1, 2).reshape(NI, KO)
    dp = (mxq(dsa, 1, "e5m2") @ mxq(wf, 1, "e4m3").T) * c
    dw = (mxq(pf, 0, "e4m3").T @ mxq(dsa, 0, "e5m2")) * c
    return dp.reshape(B, N, I), dw.reshape(N, I, K, O).transpose(0, 2, 3, 1)

@@ -1,0 +1,401 @@
+from contextlib import ExitStack
+
+import concourse.mybir as mybir
+from concourse.masks import make_identity
+
+FLOPS = 2 * 2 * 512 * 512 * 4096
+
+F32 = mybir.dt.float32
+BF16 = mybir.dt.bfloat16
+U32 = mybir.dt.uint32
+U8 = mybir.dt.uint8
+E4 = mybir.dt.float8_e4m3fn_x4
+E5 = mybir.dt.float8_e5m2_x4
+ACT = mybir.ActivationFunctionType
+ALU = mybir.AluOpType
+AX = mybir.AxisListType
+
+P = 128
+CW = 512
+NCH = 8
+NI = 512
+EPS = 1e-8
+INV_K = 1.0 / 256.0
+
+RED_PE = True
+USE_ARS = True
+MANUAL = True
+
+
+def tile_capsulenetwork_pb_v_kernel(tc, p, Wr, s, grad_out, out_0, out_1):
+    nc = tc.nc
+    s_v = s.rearrange("(p t) j o -> p t (j o)", t=4)
+    g_v = grad_out.rearrange("(p t) j o -> p t (j o)", t=4)
+    w_v = Wr.rearrange("n j o i -> n (j o) i")
+    o1_v = out_1.rearrange("n j o i -> n (j o) i")
+
+    with ExitStack() as ctx:
+        const = ctx.enter_context(tc.tile_pool(name="const", bufs=1))
+        ld = ctx.enter_context(tc.tile_pool(name="ld", bufs=4))
+        big = ctx.enter_context(tc.tile_pool(name="big", bufs=1))
+        sm = ctx.enter_context(tc.tile_pool(name="sm", bufs=2))
+        qin = ctx.enter_context(tc.tile_pool(name="qin", bufs=2))
+        cod = ctx.enter_context(tc.tile_pool(name="cod", bufs=2))
+        outp = ctx.enter_context(tc.tile_pool(name="outp", bufs=2))
+        psa = ctx.enter_context(tc.psum_pool(name="psa", bufs=1))
+        psq = ctx.enter_context(tc.psum_pool(name="psq", bufs=1))
+        psh = ctx.enter_context(tc.psum_pool(name="psh", bufs=1))
+        psw = ctx.enter_context(tc.psum_pool(name="psw", bufs=2))
+
+        ident = const.tile([P, P], F32, name="ident", tag="ident")
+        make_identity(nc, ident[:])
+        eps_t = const.tile([P, 1], F32, name="eps_t", tag="eps_t")
+        nc.vector.memset(eps_t[:], EPS)
+        one_t = const.tile([P, 1], F32, name="one_t", tag="one_t")
+        nc.vector.memset(one_t[:], 1.0)
+        warm = const.tile([P, 1], F32, name="warm", tag="warm")
+        if USE_ARS:
+            nc.scalar.activation(out=warm[:], in_=one_t[:], func=ACT.Abs_reciprocal_sqrt)
+        else:
+            nc.scalar.activation(out=warm[:], in_=one_t[:], func=ACT.Sqrt)
+
+        acc = []
+        for t in range(4):
+            acc_t = psa.tile([P, NI], F32, name="acc%d" % t, tag="acc%d" % t)
+            acc.append(acc_t)
+
+        p_codes = const.tile([P, NI], U32, name="p_codes", tag="p_codes", align_bytes=64)
+        p_sc = const.tile([P, NI], U8, name="p_sc", tag="p_sc", align_bytes=64)
+        o0 = const.tile([P, 4, NI], F32, name="o0", tag="o0")
+
+        st = {}
+
+        def ok(k):
+            return 0 <= k < NCH
+
+        def load(k):
+            if not ok(k):
+                return
+            s_t = ld.tile([P, 4, CW], F32, name="s_t", tag="s_t")
+            nc.sync.dma_start(out=s_t[:], in_=s_v[:, :, k * CW:(k + 1) * CW])
+            g_t = ld.tile([P, 4, CW], BF16, name="g_t", tag="g_t")
+            nc.sync.dma_start(out=g_t[:], in_=g_v[:, :, k * CW:(k + 1) * CW])
+            st[("s", k)] = s_t
+            st[("g", k)] = g_t
+
+        def load_w(k):
+            if not ok(k):
+                return
+            w_raw = ld.tile([P, 32, 64], BF16, name="w_raw", tag="w_raw", bufs=2)
+            nc.sync.dma_start(
+                out=w_raw[:],
+                in_=w_v[:, k * CW:(k + 1) * CW, :].rearrange("n (q t) i -> q n (t i)", t=4),
+            )
+            st[("wraw", k)] = w_raw
+
+        def prep_p():
+            p_raw = const.tile([P, 4, NI], BF16, name="p_raw", tag="p_raw")
+            nc.sync.dma_start(out=p_raw[:], in_=p.rearrange("(q t) n i -> q t (n i)", t=4))
+            st["p_raw"] = p_raw
+
+        def quant_p():
+            p_int = const.tile([P, NI, 4], BF16, name="p_int", tag="p_int", align_bytes=64)
+            nc.vector.tensor_copy(out=p_int[:], in_=st["p_raw"][:].rearrange("q t c -> q c t"))
+            nc.vector.quantize_mx(
+                out=p_codes[:].bitcast(E4), scales=p_sc[:],
+                in_=p_int[:].rearrange("q c t -> q (c t)"),
+            )
+
+        def do_sq(k):
+            if not ok(k):
+                return
+            sq = big.tile([P, 4, CW], F32, name="sq", tag="sq", bufs=2)
+            nc.scalar.activation(out=sq[:], in_=st[("s", k)][:], func=ACT.Square)
+            st[("sq", k)] = sq
+
+        def do_tg(k):
+            if not ok(k):
+                return
+            tg = big.tile([P, 4, CW], F32, name="tg", tag="tg", bufs=2)
+            for hh in range(2):
+                nc.vector.tensor_tensor(
+                    out=tg[:, 2 * hh:2 * hh + 2, :],
+                    in0=st[("s", k)][:, 2 * hh:2 * hh + 2, :],
+                    in1=st[("g", k)][:, 2 * hh:2 * hh + 2, :],
+                    op=ALU.mult,
+                )
+            st[("tg", k)] = tg
+
+        def red(k):
+            if not ok(k):
+                return
+            srcs = (st[("sq", k)], st[("tg", k)])
+            if RED_PE:
+                qd = psq.tile([P, 2, P], F32, name="qd", tag="qd")
+                for w in range(2):
+                    view = srcs[w][:].rearrange("q t (j o) -> q (t j) o", o=16)
+                    for o in range(16):
+                        nc.tensor.matmul(
+                            out=qd[:, w, :], lhsT=view[:, :, o], rhs=ident[:],
+                            is_transpose=True, start=(o == 0), stop=(o == 15),
+                        )
+            else:
+                qd = sm.tile([P, 2, P], F32, name="qds", tag="qds")
+                for w in range(2):
+                    nc.vector.tensor_reduce(
+                        out=qd[:, w, :],
+                        in_=srcs[w][:].rearrange("q t (j o) -> q (t j) o", o=16),
+                        axis=AX.X, op=ALU.add,
+                    )
+            st[("qd", k)] = qd
+
+        def smt(k, nm):
+            tl = sm.tile([P, P], F32, name=nm, tag=nm)
+            st[(nm, k)] = tl
+            return tl
+
+        def sm_s1(k):
+            if not ok(k):
+                return
+            q = st[("qd", k)][:, 0, :]
+            r = smt(k, "r")
+            if USE_ARS:
+                nc.scalar.activation(out=r[:], in_=q, func=ACT.Abs_reciprocal_sqrt, bias=eps_t[:, 0:1])
+            else:
+                rt = smt(k, "rt")
+                nc.scalar.activation(out=rt[:], in_=q, func=ACT.Sqrt, bias=eps_t[:, 0:1])
+            q1 = smt(k, "q1")
+            nc.scalar.activation(out=q1[:], in_=q, func=ACT.Identity, bias=one_t[:, 0:1])
+
+        def sm_w(k):
+            if not ok(k):
+                return
+            if not USE_ARS:
+                nc.vector.reciprocal(out=st[("r", k)][:], in_=st[("rt", k)][:])
+            w = smt(k, "w")
+            nc.vector.reciprocal(out=w[:], in_=st[("q1", k)][:])
+
+        def sm_a(k):
+            if not ok(k):
+                return
+            a = smt(k, "a")
+            nc.vector.tensor_tensor(out=a[:], in0=st[("r", k)][:], in1=st[("w", k)][:], op=ALU.mult)
+
+        def sm_s2(k):
+            if not ok(k):
+                return
+            a2 = smt(k, "a2")
+            nc.scalar.activation(out=a2[:], in_=st[("a", k)][:], func=ACT.Square)
+
+        def sm_n1(k):
+            if not ok(k):
+                return
+            n1 = smt(k, "n1")
+            nc.vector.scalar_tensor_tensor(
+                out=n1[:], in0=st[("q1", k)][:], scalar=2.0, in1=st[("qd", k)][:, 0, :],
+                op0=ALU.subtract, op1=ALU.mult,
+            )
+
+        def sm_nd(k):
+            if not ok(k):
+                return
+            nd = smt(k, "nd")
+            nc.vector.scalar_tensor_tensor(
+                out=nd[:], in0=st[("n1", k)][:], scalar=2.0 * EPS, in1=st[("qd", k)][:, 1, :],
+                op0=ALU.subtract, op1=ALU.mult,
+            )
+
+        def sm_h(k):
+            if not ok(k):
+                return
+            hc = sm.tile([P, 2, P], F32, name="hc", tag="hc")
+            st[("hc", k)] = hc
+            nc.vector.tensor_tensor(out=hc[:, 0, :], in0=st[("qd", k)][:, 0, :], in1=st[("a", k)][:], op=ALU.mult)
+
+        def sm_ar(k):
+            if not ok(k):
+                return
+            ar = smt(k, "ar")
+            nc.vector.tensor_tensor(out=ar[:], in0=st[("a2", k)][:], in1=st[("r", k)][:], op=ALU.mult)
+
+        def sm_c(k):
+            if not ok(k):
+                return
+            nc.vector.scalar_tensor_tensor(
+                out=st[("hc", k)][:, 1, :], in0=st[("nd", k)][:], scalar=-1.0, in1=st[("ar", k)][:],
+                op0=ALU.mult, op1=ALU.mult,
+            )
+
+        def back(k):
+            if not ok(k):
+                return
+            if RED_PE:
+                hp = psh.tile([P, 2, P], F32, name="hp", tag="hp")
+                for w in range(2):
+                    nc.tensor.transpose(out=hp[:, w, :], in_=st[("hc", k)][:, w, :], identity=ident[:])
+                st[("hp", k)] = hp
+            else:
+                st[("hp", k)] = st[("hc", k)]
+
+        def prod(k, w, hh):
+            if not ok(k):
+                return
+            nm = ("pa", "pb")[w]
+            if hh == 0:
+                tl = big.tile([P, 4, CW], F32, name=nm, tag=nm)
+                st[(nm, k)] = tl
+            tl = st[(nm, k)]
+            src = st[(("g", "s")[w], k)]
+            nc.vector.tensor_tensor(
+                out=tl[:, 2 * hh:2 * hh + 2, :].rearrange("q t (j o) -> q (t j) o", o=16),
+                in0=st[("hp", k)][:, w, 64 * hh:64 * hh + 64].unsqueeze(2).to_broadcast([P, 64, 16]),
+                in1=src[:, 2 * hh:2 * hh + 2, :].rearrange("q t (j o) -> q (t j) o", o=16),
+                op=ALU.mult,
+            )
+
+        def add(k, u):
+            if not ok(k):
+                return
+            if u == 0:
+                ds = qin.tile([P, 4, 2, 256], BF16, name="ds", tag="ds", align_bytes=64)
+                st[("ds", k)] = ds
+            ds = st[("ds", k)]
+            nc.vector.tensor_tensor(
+                out=ds[:, :, u, :].rearrange("q t (m e) -> q t m e", e=2),
+                in0=st[("pa", k)][:].rearrange("q t (m u e) -> q u t m e", u=2, e=2)[:, u],
+                in1=st[("pb", k)][:].rearrange("q t (m u e) -> q u t m e", u=2, e=2)[:, u],
+                op=ALU.add,
+            )
+
+        def tr(k):
+            if not ok(k):
+                return
+            dsw = st[("ds", k)][:].rearrange("q t u x -> q (t u x)").bitcast(F32).rearrange(
+                "q (t u m) -> q t u m", t=4, u=2)
+            dst_in = qin.tile([P, NI, 4], BF16, name="dst_in", tag="dst_in", align_bytes=64)
+            st[("dst_in", k)] = dst_in
+            dww = dst_in[:].rearrange("q c k -> q (c k)").bitcast(F32).rearrange(
+                "q (t m u) -> q t m u", t=4, u=2)
+            for hh in range(2):
+                tp = psw.tile([P, 2, 2, P], F32, name="tp", tag="w")
+                for tt in range(2):
+                    for u in range(2):
+                        nc.tensor.transpose(out=tp[:, tt, u, :], in_=dsw[:, 2 * hh + tt, u, :], identity=ident[:])
+                nc.scalar.copy(out=dww[:, 2 * hh:2 * hh + 2, :, :], in_=tp[:].rearrange("q t u m -> q t m u"))
+
+        def il(k, u):
+            if not ok(k):
+                return
+            if u == 0:
+                ds_int = qin.tile([P, NI, 4], BF16, name="ds_int", tag="ds_int", align_bytes=64)
+                st[("ds_int", k)] = ds_int
+            ds_int = st[("ds_int", k)]
+            nc.vector.tensor_copy(
+                out=ds_int[:, u * 256:(u + 1) * 256, :].rearrange("q (e m) t -> q e m t", e=2),
+                in_=st[("ds", k)][:, :, u, :].rearrange("q t (m e) -> q e m t", e=2),
+            )
+
+        def quant(k, src, dstn, fmt):
+            if not ok(k):
+                return
+            c_t = cod.tile([P, NI], U32, name=dstn + "_c", tag=dstn + "_c", align_bytes=64)
+            s_t = cod.tile([P, NI], U8, name=dstn + "_s", tag=dstn + "_s", align_bytes=64)
+            nc.vector.quantize_mx(
+                out=c_t[:].bitcast(fmt), scales=s_t[:],
+                in_=st[(src, k)][:].rearrange("q c t -> q (c t)"),
+            )
+            st[(dstn + "_c", k)] = c_t
+            st[(dstn + "_s", k)] = s_t
+
+        def w_int(k):
+            if not ok(k):
+                return
+            wi = qin.tile([P, NI, 4], BF16, name="wi", tag="wi", align_bytes=64)
+            nc.scalar.copy(
+                out=wi[:].rearrange("q (n i) t -> q n i t", i=16),
+                in_=st[("wraw", k)][:].rearrange("q n (t i) -> q n i t", t=4),
+            )
+            st[("wi", k)] = wi
+
+        def mm1(k):
+            if not ok(k):
+                return
+            o1 = outp.tile([P, 32, 4, 16], F32, name="o1", tag="o1")
+            for a in range(4):
+                ot = psw.tile([P, NI], F32, name="ot", tag="w")
+                nc.tensor.matmul_mx(
+                    out=ot[:],
+                    lhsT=st[("dsq_c", k)][:, a * P:(a + 1) * P].bitcast(E5),
+                    lhsT_scale=st[("dsq_s", k)][:, a * P:(a + 1) * P],
+                    rhs=p_codes[:].bitcast(E4), rhs_scale=p_sc[:],
+                    start=True, stop=True,
+                )
+                nc.scalar.activation(
+                    out=o1[:, :, a, :], in_=ot[:].rearrange("q (n i) -> q n i", i=16),
+                    func=ACT.Copy, scale=INV_K,
+                )
+            nc.scalar.dma_start(
+                out=o1_v[:, k * CW:(k + 1) * CW, :].rearrange("n (m a) i -> m n (a i)", a=4),
+                in_=o1[:].rearrange("q n a i -> q n (a i)"),
+            )
+
+        def mm0(k):
+            if not ok(k):
+                return
+            for t in range(4):
+                nc.tensor.matmul_mx(
+                    out=acc[t][:],
+                    lhsT=st[("dtq_c", k)][:, t * P:(t + 1) * P].bitcast(E5),
+                    lhsT_scale=st[("dtq_s", k)][:, t * P:(t + 1) * P],
+                    rhs=st[("wq_c", k)][:].bitcast(E4), rhs_scale=st[("wq_s", k)][:],
+                    start=(k == 0), stop=(k == NCH - 1),
+                )
+
+        def body():
+            for i in range(-3, NCH + 1):
+                load(i + 3)
+                load_w(i + 2)
+                if i == -2:
+                    prep_p()
+                mm1(i - 1)
+                mm0(i - 1)
+                do_sq(i + 2)
+                do_tg(i + 1)
+                red(i + 1)
+                if i == -1:
+                    quant_p()
+                w_int(i + 1)
+                sm_s1(i + 1)
+                prod(i, 0, 0)
+                prod(i, 0, 1)
+                prod(i, 1, 0)
+                prod(i, 1, 1)
+                add(i, 0)
+                sm_w(i + 1)
+                add(i, 1)
+                sm_a(i + 1)
+                sm_s2(i + 1)
+                tr(i)
+                il(i, 0)
+                sm_n1(i + 1)
+                il(i, 1)
+                sm_nd(i + 1)
+                quant(i, "ds_int", "dsq", E5)
+                sm_h(i + 1)
+                quant(i + 1, "wi", "wq", E4)
+                sm_ar(i + 1)
+                quant(i, "dst_in", "dtq", E5)
+                sm_c(i + 1)
+                back(i + 1)
+            for t in range(4):
+                if t < 2:
+                    nc.scalar.activation(out=o0[:, t, :], in_=acc[t][:], func=ACT.Copy, scale=INV_K)
+                else:
+                    nc.vector.tensor_scalar_mul(out=o0[:, t, :], in0=acc[t][:], scalar1=INV_K)
+            nc.sync.dma_start(out=out_0.rearrange("(q t) n i -> q t (n i)", t=4), in_=o0[:])
+
+        if MANUAL:
+            with tc.manual_schedule():
+                body()
+        else:
+            body()

@@ -22,8 +22,8 @@ NI = 512
 EPS = 1e-8
 INV_K = 1.0 / 256.0
 
-RED_PE = True
-USE_ARS = True
+TG_ON_G = True
+TG_OMAJOR = False
 MANUAL = True
 
 
@@ -54,10 +54,7 @@ def tile_capsulenetwork_pb_v_kernel(tc, p, Wr, s, grad_out, out_0, out_1):
         one_t = const.tile([P, 1], F32, name="one_t", tag="one_t")
         nc.vector.memset(one_t[:], 1.0)
         warm = const.tile([P, 1], F32, name="warm", tag="warm")
-        if USE_ARS:
-            nc.scalar.activation(out=warm[:], in_=one_t[:], func=ACT.Abs_reciprocal_sqrt)
-        else:
-            nc.scalar.activation(out=warm[:], in_=one_t[:], func=ACT.Sqrt)
+        nc.scalar.activation(out=warm[:], in_=one_t[:], func=ACT.Abs_reciprocal_sqrt)
 
         acc = []
         for t in range(4):
@@ -77,9 +74,14 @@ def tile_capsulenetwork_pb_v_kernel(tc, p, Wr, s, grad_out, out_0, out_1):
             if not ok(k):
                 return
             s_t = ld.tile([P, 4, CW], F32, name="s_t", tag="s_t")
-            nc.sync.dma_start(out=s_t[:], in_=s_v[:, :, k * CW:(k + 1) * CW])
             g_t = ld.tile([P, 4, CW], BF16, name="g_t", tag="g_t")
-            nc.sync.dma_start(out=g_t[:], in_=g_v[:, :, k * CW:(k + 1) * CW])
+            if k == 0:
+                for hh in range(2):
+                    nc.sync.dma_start(out=s_t[:, 2 * hh:2 * hh + 2, :], in_=s_v[:, 2 * hh:2 * hh + 2, 0:CW])
+                    nc.sync.dma_start(out=g_t[:, 2 * hh:2 * hh + 2, :], in_=g_v[:, 2 * hh:2 * hh + 2, 0:CW])
+            else:
+                nc.sync.dma_start(out=s_t[:], in_=s_v[:, :, k * CW:(k + 1) * CW])
+                nc.sync.dma_start(out=g_t[:], in_=g_v[:, :, k * CW:(k + 1) * CW])
             st[("s", k)] = s_t
             st[("g", k)] = g_t
 
@@ -98,9 +100,13 @@ def tile_capsulenetwork_pb_v_kernel(tc, p, Wr, s, grad_out, out_0, out_1):
             nc.sync.dma_start(out=p_raw[:], in_=p.rearrange("(q t) n i -> q t (n i)", t=4))
             st["p_raw"] = p_raw
 
-        def quant_p():
+        def il_p():
             p_int = const.tile([P, NI, 4], BF16, name="p_int", tag="p_int", align_bytes=64)
-            nc.vector.tensor_copy(out=p_int[:], in_=st["p_raw"][:].rearrange("q t c -> q c t"))
+            nc.scalar.copy(out=p_int[:], in_=st["p_raw"][:].rearrange("q t c -> q c t"))
+            st["p_int"] = p_int
+
+        def quant_p():
+            p_int = st["p_int"]
             nc.vector.quantize_mx(
                 out=p_codes[:].bitcast(E4), scales=p_sc[:],
                 in_=p_int[:].rearrange("q c t -> q (c t)"),
@@ -109,45 +115,69 @@ def tile_capsulenetwork_pb_v_kernel(tc, p, Wr, s, grad_out, out_0, out_1):
         def do_sq(k):
             if not ok(k):
                 return
-            sq = big.tile([P, 4, CW], F32, name="sq", tag="sq", bufs=2)
-            nc.scalar.activation(out=sq[:], in_=st[("s", k)][:], func=ACT.Square)
+            sq = big.tile([P, 16, P], F32, name="sq", tag="sq", bufs=2)
+            if k == 0:
+                for hh in range(2):
+                    nc.scalar.activation(
+                        out=sq[:, :, 64 * hh:64 * hh + 64].rearrange("q (a b) c -> q a c b", a=4),
+                        in_=st[("s", k)][:, 2 * hh:2 * hh + 2, :].rearrange("q t (j a b) -> q a (t j) b", a=4, b=4),
+                        func=ACT.Square,
+                    )
+            else:
+                nc.scalar.activation(
+                    out=sq[:].rearrange("q (a b) c -> q a c b", a=4),
+                    in_=st[("s", k)][:].rearrange("q t (j a b) -> q a (t j) b", a=4, b=4),
+                    func=ACT.Square,
+                )
             st[("sq", k)] = sq
 
-        def do_tg(k):
+        def do_tg(k, on_g):
             if not ok(k):
                 return
             tg = big.tile([P, 4, CW], F32, name="tg", tag="tg", bufs=2)
-            for hh in range(2):
-                nc.vector.tensor_tensor(
-                    out=tg[:, 2 * hh:2 * hh + 2, :],
-                    in0=st[("s", k)][:, 2 * hh:2 * hh + 2, :],
-                    in1=st[("g", k)][:, 2 * hh:2 * hh + 2, :],
-                    op=ALU.mult,
-                )
             st[("tg", k)] = tg
+            if on_g:
+                nc.vector.memset(tg[:, 0, 0:1], 0.0)
+                nc.gpsimd.tensor_tensor(out=tg[:], in0=st[("s", k)][:], in1=st[("g", k)][:], op=ALU.mult)
+                return
+            for hh in range(2):
+                if TG_OMAJOR:
+                    out_ap = tg[:].rearrange("q t x -> q (t x)").rearrange("q (o c) -> q o c", o=16)[
+                        :, :, 64 * hh:64 * hh + 64].rearrange("q (a b) c -> q a c b", a=4)
+                    nc.vector.tensor_tensor(
+                        out=out_ap,
+                        in0=st[("s", k)][:, 2 * hh:2 * hh + 2, :].rearrange("q t (j a b) -> q a (t j) b", a=4, b=4),
+                        in1=st[("g", k)][:, 2 * hh:2 * hh + 2, :].rearrange("q t (j a b) -> q a (t j) b", a=4, b=4),
+                        op=ALU.mult,
+                    )
+                else:
+                    nc.vector.tensor_tensor(
+                        out=tg[:, 2 * hh:2 * hh + 2, :],
+                        in0=st[("s", k)][:, 2 * hh:2 * hh + 2, :],
+                        in1=st[("g", k)][:, 2 * hh:2 * hh + 2, :],
+                        op=ALU.mult,
+                    )
 
         def red(k):
             if not ok(k):
                 return
-            srcs = (st[("sq", k)], st[("tg", k)])
-            if RED_PE:
-                qd = psq.tile([P, 2, P], F32, name="qd", tag="qd")
-                for w in range(2):
-                    view = srcs[w][:].rearrange("q t (j o) -> q (t j) o", o=16)
-                    for o in range(16):
-                        nc.tensor.matmul(
-                            out=qd[:, w, :], lhsT=view[:, :, o], rhs=ident[:],
-                            is_transpose=True, start=(o == 0), stop=(o == 15),
-                        )
-            else:
-                qd = sm.tile([P, 2, P], F32, name="qds", tag="qds")
-                for w in range(2):
-                    nc.vector.tensor_reduce(
-                        out=qd[:, w, :],
-                        in_=srcs[w][:].rearrange("q t (j o) -> q (t j) o", o=16),
-                        axis=AX.X, op=ALU.add,
-                    )
+            qd = psq.tile([P, 2, P], F32, name="qd", tag="qd")
             st[("qd", k)] = qd
+            sq = st[("sq", k)]
+            for o in range(16):
+                nc.tensor.matmul(
+                    out=qd[:, 0, :], lhsT=sq[:, o, :], rhs=ident[:],
+                    is_transpose=True, start=(o == 0), stop=(o == 15),
+                )
+            if TG_OMAJOR:
+                view = st[("tg", k)][:].rearrange("q t x -> q (t x)").rearrange("q (o c) -> q c o", o=16)
+            else:
+                view = st[("tg", k)][:].rearrange("q t (j o) -> q (t j) o", o=16)
+            for o in range(16):
+                nc.tensor.matmul(
+                    out=qd[:, 1, :], lhsT=view[:, :, o], rhs=ident[:],
+                    is_transpose=True, start=(o == 0), stop=(o == 15),
+                )
 
         def smt(k, nm):
             tl = sm.tile([P, P], F32, name=nm, tag=nm)
@@ -158,51 +188,39 @@ def tile_capsulenetwork_pb_v_kernel(tc, p, Wr, s, grad_out, out_0, out_1):
             if not ok(k):
                 return
             q = st[("qd", k)][:, 0, :]
-            r = smt(k, "r")
-            if USE_ARS:
-                nc.scalar.activation(out=r[:], in_=q, func=ACT.Abs_reciprocal_sqrt, bias=eps_t[:, 0:1])
-            else:
-                rt = smt(k, "rt")
-                nc.scalar.activation(out=rt[:], in_=q, func=ACT.Sqrt, bias=eps_t[:, 0:1])
-            q1 = smt(k, "q1")
-            nc.scalar.activation(out=q1[:], in_=q, func=ACT.Identity, bias=one_t[:, 0:1])
+            nc.scalar.activation(out=smt(k, "r")[:], in_=q, func=ACT.Abs_reciprocal_sqrt, bias=eps_t[:, 0:1])
+            nc.scalar.activation(out=smt(k, "v")[:], in_=q, func=ACT.Abs_reciprocal_sqrt, bias=one_t[:, 0:1])
+            nc.scalar.copy(out=smt(k, "qs")[:], in_=q)
+            nc.scalar.copy(out=smt(k, "dt")[:], in_=st[("qd", k)][:, 1, :])
+            nc.scalar.activation(out=smt(k, "w")[:], in_=st[("v", k)][:], func=ACT.Square)
 
-        def sm_w(k):
+        def tt(k, nm, x, y):
             if not ok(k):
                 return
-            if not USE_ARS:
-                nc.vector.reciprocal(out=st[("r", k)][:], in_=st[("rt", k)][:])
-            w = smt(k, "w")
-            nc.vector.reciprocal(out=w[:], in_=st[("q1", k)][:])
-
-        def sm_a(k):
-            if not ok(k):
-                return
-            a = smt(k, "a")
-            nc.vector.tensor_tensor(out=a[:], in0=st[("r", k)][:], in1=st[("w", k)][:], op=ALU.mult)
-
-        def sm_s2(k):
-            if not ok(k):
-                return
-            a2 = smt(k, "a2")
-            nc.scalar.activation(out=a2[:], in_=st[("a", k)][:], func=ACT.Square)
+            nc.vector.tensor_tensor(out=smt(k, nm)[:], in0=st[(x, k)][:], in1=st[(y, k)][:], op=ALU.mult)
 
         def sm_n1(k):
             if not ok(k):
                 return
-            n1 = smt(k, "n1")
             nc.vector.scalar_tensor_tensor(
-                out=n1[:], in0=st[("q1", k)][:], scalar=2.0, in1=st[("qd", k)][:, 0, :],
+                out=smt(k, "n1")[:], in0=st[("qs", k)][:], scalar=1.0, in1=st[("qs", k)][:],
                 op0=ALU.subtract, op1=ALU.mult,
             )
 
         def sm_nd(k):
             if not ok(k):
                 return
-            nd = smt(k, "nd")
             nc.vector.scalar_tensor_tensor(
-                out=nd[:], in0=st[("n1", k)][:], scalar=2.0 * EPS, in1=st[("qd", k)][:, 1, :],
+                out=smt(k, "nd")[:], in0=st[("n1", k)][:], scalar=2.0 * EPS, in1=st[("dt", k)][:],
                 op0=ALU.subtract, op1=ALU.mult,
+            )
+
+        def sm_na(k):
+            if not ok(k):
+                return
+            nc.vector.scalar_tensor_tensor(
+                out=smt(k, "na")[:], in0=st[("nd", k)][:], scalar=-1.0, in1=st[("a", k)][:],
+                op0=ALU.mult, op1=ALU.mult,
             )
 
         def sm_h(k):
@@ -210,32 +228,20 @@ def tile_capsulenetwork_pb_v_kernel(tc, p, Wr, s, grad_out, out_0, out_1):
                 return
             hc = sm.tile([P, 2, P], F32, name="hc", tag="hc")
             st[("hc", k)] = hc
-            nc.vector.tensor_tensor(out=hc[:, 0, :], in0=st[("qd", k)][:, 0, :], in1=st[("a", k)][:], op=ALU.mult)
-
-        def sm_ar(k):
-            if not ok(k):
-                return
-            ar = smt(k, "ar")
-            nc.vector.tensor_tensor(out=ar[:], in0=st[("a2", k)][:], in1=st[("r", k)][:], op=ALU.mult)
+            nc.vector.tensor_tensor(out=hc[:, 0, :], in0=st[("qs", k)][:], in1=st[("a", k)][:], op=ALU.mult)
 
         def sm_c(k):
             if not ok(k):
                 return
-            nc.vector.scalar_tensor_tensor(
-                out=st[("hc", k)][:, 1, :], in0=st[("nd", k)][:], scalar=-1.0, in1=st[("ar", k)][:],
-                op0=ALU.mult, op1=ALU.mult,
-            )
+            nc.vector.tensor_tensor(out=st[("hc", k)][:, 1, :], in0=st[("na", k)][:], in1=st[("b", k)][:], op=ALU.mult)
 
         def back(k):
             if not ok(k):
                 return
-            if RED_PE:
-                hp = psh.tile([P, 2, P], F32, name="hp", tag="hp")
-                for w in range(2):
-                    nc.tensor.transpose(out=hp[:, w, :], in_=st[("hc", k)][:, w, :], identity=ident[:])
-                st[("hp", k)] = hp
-            else:
-                st[("hp", k)] = st[("hc", k)]
+            hp = psh.tile([P, 2, P], F32, name="hp", tag="hp")
+            for w in range(2):
+                nc.tensor.transpose(out=hp[:, w, :], in_=st[("hc", k)][:, w, :], identity=ident[:])
+            st[("hp", k)] = hp
 
         def prod(k, w, hh):
             if not ok(k):
@@ -330,10 +336,14 @@ def tile_capsulenetwork_pb_v_kernel(tc, p, Wr, s, grad_out, out_0, out_1):
                     rhs=p_codes[:].bitcast(E4), rhs_scale=p_sc[:],
                     start=True, stop=True,
                 )
-                nc.scalar.activation(
-                    out=o1[:, :, a, :], in_=ot[:].rearrange("q (n i) -> q n i", i=16),
-                    func=ACT.Copy, scale=INV_K,
-                )
+                if k == NCH - 1 and a % 2 == 1:
+                    nc.vector.tensor_scalar_mul(
+                        out=o1[:, :, a, :], in0=ot[:].rearrange("q (n i) -> q n i", i=16), scalar1=INV_K)
+                else:
+                    nc.scalar.activation(
+                        out=o1[:, :, a, :], in_=ot[:].rearrange("q (n i) -> q n i", i=16),
+                        func=ACT.Copy, scale=INV_K,
+                    )
             nc.scalar.dma_start(
                 out=o1_v[:, k * CW:(k + 1) * CW, :].rearrange("n (m a) i -> m n (a i)", a=4),
                 in_=o1[:].rearrange("q n a i -> q n (a i)"),
@@ -354,39 +364,40 @@ def tile_capsulenetwork_pb_v_kernel(tc, p, Wr, s, grad_out, out_0, out_1):
         def body():
             for i in range(-3, NCH + 1):
                 load(i + 3)
-                load_w(i + 2)
                 if i == -2:
                     prep_p()
+                load_w(i + 2)
+                do_sq(i + 2)
+                red(i + 1)
+                sm_s1(i + 1)
+                if i == -1:
+                    il_p()
                 mm1(i - 1)
                 mm0(i - 1)
-                do_sq(i + 2)
-                do_tg(i + 1)
-                red(i + 1)
-                if i == -1:
-                    quant_p()
-                w_int(i + 1)
-                sm_s1(i + 1)
+                do_tg(i + 2, TG_ON_G and i >= 0)
                 prod(i, 0, 0)
                 prod(i, 0, 1)
                 prod(i, 1, 0)
                 prod(i, 1, 1)
                 add(i, 0)
-                sm_w(i + 1)
+                tt(i + 1, "a", "r", "w")
                 add(i, 1)
-                sm_a(i + 1)
-                sm_s2(i + 1)
+                sm_n1(i + 1)
                 tr(i)
                 il(i, 0)
-                sm_n1(i + 1)
+                tt(i + 1, "b", "a", "r")
                 il(i, 1)
                 sm_nd(i + 1)
-                quant(i, "ds_int", "dsq", E5)
                 sm_h(i + 1)
-                quant(i + 1, "wi", "wq", E4)
-                sm_ar(i + 1)
-                quant(i, "dst_in", "dtq", E5)
+                quant(i, "ds_int", "dsq", E5)
+                sm_na(i + 1)
+                if i == 0:
+                    quant_p()
+                quant(i, "wi", "wq", E4)
                 sm_c(i + 1)
+                quant(i, "dst_in", "dtq", E5)
                 back(i + 1)
+                w_int(i + 1)
             for t in range(4):
                 if t < 2:
                     nc.scalar.activation(out=o0[:, t, :], in_=acc[t][:], func=ACT.Copy, scale=INV_K)

@@ -22,9 +22,10 @@ NI = 512
 EPS = 1e-8
 INV_K = 1.0 / 256.0
 
-TG_ON_G = True
-TG_OMAJOR = False
+IL_ON_S = True
 MANUAL = True
+GROUPS = ((0, 1), (2, 3), (4, 5), (6,), (7,))
+MM1_PLAN = {2: ((0, 0, 4),), 3: ((0, 4, 8),), 4: ((1, 0, 4),), 5: ((1, 4, 8),), 6: ((2, 0, 8),), 7: ((3, 0, 4),), 8: ((4, 0, 4),)}
 
 
 def tile_capsulenetwork_pb_v_kernel(tc, p, Wr, s, grad_out, out_0, out_1):
@@ -141,7 +142,7 @@ def tile_capsulenetwork_pb_v_kernel(tc, p, Wr, s, grad_out, out_0, out_1):
                 nc.gpsimd.tensor_tensor(out=tg[:], in0=st[("s", k)][:], in1=st[("g", k)][:], op=ALU.mult)
                 return
             for hh in range(2):
-                if TG_OMAJOR:
+                if True:
                     out_ap = tg[:].rearrange("q t x -> q (t x)").rearrange("q (o c) -> q o c", o=16)[
                         :, :, 64 * hh:64 * hh + 64].rearrange("q (a b) c -> q a c b", a=4)
                     nc.vector.tensor_tensor(
@@ -169,7 +170,7 @@ def tile_capsulenetwork_pb_v_kernel(tc, p, Wr, s, grad_out, out_0, out_1):
                     out=qd[:, 0, :], lhsT=sq[:, o, :], rhs=ident[:],
                     is_transpose=True, start=(o == 0), stop=(o == 15),
                 )
-            if TG_OMAJOR:
+            if k < 2:
                 view = st[("tg", k)][:].rearrange("q t x -> q (t x)").rearrange("q (o c) -> q c o", o=16)
             else:
                 view = st[("tg", k)][:].rearrange("q t (j o) -> q (t j) o", o=16)
@@ -289,17 +290,45 @@ def tile_capsulenetwork_pb_v_kernel(tc, p, Wr, s, grad_out, out_0, out_1):
                         nc.tensor.transpose(out=tp[:, tt, u, :], in_=dsw[:, 2 * hh + tt, u, :], identity=ident[:])
                 nc.scalar.copy(out=dww[:, 2 * hh:2 * hh + 2, :, :], in_=tp[:].rearrange("q t u m -> q t m u"))
 
-        def il(k, u):
+        def grp_of(k):
+            for gi in range(len(GROUPS)):
+                if k in GROUPS[gi]:
+                    return gi, GROUPS[gi].index(k), len(GROUPS[gi])
+            return None
+
+        def il(k, u, on_s):
             if not ok(k):
                 return
-            if u == 0:
-                ds_int = qin.tile([P, NI, 4], BF16, name="ds_int", tag="ds_int", align_bytes=64)
-                st[("ds_int", k)] = ds_int
-            ds_int = st[("ds_int", k)]
-            nc.vector.tensor_copy(
-                out=ds_int[:, u * 256:(u + 1) * 256, :].rearrange("q (e m) t -> q e m t", e=2),
-                in_=st[("ds", k)][:, :, u, :].rearrange("q t (m e) -> q e m t", e=2),
+            gi, gam, gn = grp_of(k)
+            if ("ds_int", gi) not in st:
+                ds_int = qin.tile([P, 2 * NI, 4], BF16, name="ds_int", tag="ds_int", align_bytes=64)
+                st[("ds_int", gi)] = ds_int
+            ds_int = st[("ds_int", gi)]
+            mw = P // gn
+            for lam in range(gn):
+                a0 = 4 * lam + 2 * u
+                out_ap = ds_int[:, 0:NI * gn, :].rearrange("q (a m) t -> q a m t", m=P)[
+                    :, a0:a0 + 2, mw * gam:mw * (gam + 1), :]
+                in_ap = st[("ds", k)][:, :, u, :].rearrange("q t (m l e) -> q l e m t", l=gn, e=2)[:, lam]
+                if on_s:
+                    nc.scalar.copy(out=out_ap, in_=in_ap)
+                else:
+                    nc.vector.tensor_copy(out=out_ap, in_=in_ap)
+
+        def quant_ds(k):
+            if not ok(k):
+                return
+            gi, gam, gn = grp_of(k)
+            if gam != gn - 1:
+                return
+            c_t = cod.tile([P, 2 * NI], U32, name="dsq_c", tag="dsq_c", align_bytes=64)
+            s_t = cod.tile([P, 2 * NI], U8, name="dsq_s", tag="dsq_s", align_bytes=64)
+            nc.vector.quantize_mx(
+                out=c_t[:, 0:NI * gn].bitcast(E5), scales=s_t[:, 0:NI * gn],
+                in_=st[("ds_int", gi)][:, 0:NI * gn, :].rearrange("q c t -> q (c t)"),
             )
+            st[("dsq_c", gi)] = c_t
+            st[("dsq_s", gi)] = s_t
 
         def quant(k, src, dstn, fmt):
             if not ok(k):
@@ -322,32 +351,38 @@ def tile_capsulenetwork_pb_v_kernel(tc, p, Wr, s, grad_out, out_0, out_1):
                 in_=st[("wraw", k)][:].rearrange("q n (t i) -> q n i t", t=4),
             )
             st[("wi", k)] = wi
+            load_w(k + 2)
 
-        def mm1(k):
-            if not ok(k):
-                return
-            o1 = outp.tile([P, 32, 4, 16], F32, name="o1", tag="o1")
-            for a in range(4):
-                ot = psw.tile([P, NI], F32, name="ot", tag="w")
-                nc.tensor.matmul_mx(
-                    out=ot[:],
-                    lhsT=st[("dsq_c", k)][:, a * P:(a + 1) * P].bitcast(E5),
-                    lhsT_scale=st[("dsq_s", k)][:, a * P:(a + 1) * P],
-                    rhs=p_codes[:].bitcast(E4), rhs_scale=p_sc[:],
-                    start=True, stop=True,
-                )
-                if k == NCH - 1 and a % 2 == 1:
-                    nc.vector.tensor_scalar_mul(
-                        out=o1[:, :, a, :], in0=ot[:].rearrange("q (n i) -> q n i", i=16), scalar1=INV_K)
-                else:
-                    nc.scalar.activation(
-                        out=o1[:, :, a, :], in_=ot[:].rearrange("q (n i) -> q n i", i=16),
-                        func=ACT.Copy, scale=INV_K,
+        def mm1(step):
+            for gi, a_lo, a_hi in MM1_PLAN.get(step, ()):
+                gn = len(GROUPS[gi])
+                if a_lo == 0:
+                    o1 = outp.tile([P, 32, 8, 16], F32, name="o1", tag="o1")
+                    st[("o1", gi)] = o1
+                o1 = st[("o1", gi)]
+                for a in range(a_lo, a_hi):
+                    ot = psw.tile([P, NI], F32, name="ot", tag="w")
+                    nc.tensor.matmul_mx(
+                        out=ot[:],
+                        lhsT=st[("dsq_c", gi)][:, a * P:(a + 1) * P].bitcast(E5),
+                        lhsT_scale=st[("dsq_s", gi)][:, a * P:(a + 1) * P],
+                        rhs=p_codes[:].bitcast(E4), rhs_scale=p_sc[:],
+                        start=True, stop=True,
                     )
-            nc.scalar.dma_start(
-                out=o1_v[:, k * CW:(k + 1) * CW, :].rearrange("n (m a) i -> m n (a i)", a=4),
-                in_=o1[:].rearrange("q n a i -> q n (a i)"),
-            )
+                    if gi == len(GROUPS) - 1 and a % 2 == 1:
+                        nc.vector.tensor_scalar_mul(
+                            out=o1[:, :, a, :], in0=ot[:].rearrange("q (n i) -> q n i", i=16), scalar1=INV_K)
+                    else:
+                        nc.scalar.activation(
+                            out=o1[:, :, a, :], in_=ot[:].rearrange("q (n i) -> q n i", i=16),
+                            func=ACT.Copy, scale=INV_K,
+                        )
+                if a_hi == 4 * gn:
+                    lo = GROUPS[gi][0] * CW
+                    nc.scalar.dma_start(
+                        out=o1_v[:, lo:lo + gn * CW, :].rearrange("n (m a) i -> m n (a i)", a=4 * gn),
+                        in_=o1[:, :, 0:4 * gn, :].rearrange("q n a i -> q n (a i)"),
+                    )
 
         def mm0(k):
             if not ok(k):
@@ -363,18 +398,25 @@ def tile_capsulenetwork_pb_v_kernel(tc, p, Wr, s, grad_out, out_0, out_1):
 
         def body():
             for i in range(-3, NCH + 1):
-                load(i + 3)
-                if i == -2:
+                if i == -3:
+                    load(0)
+                    load(1)
+                    load(2)
+                    load_w(0)
                     prep_p()
-                load_w(i + 2)
+                    load(3)
+                    load_w(1)
+                elif i > 0:
+                    load(i + 3)
                 do_sq(i + 2)
                 red(i + 1)
                 sm_s1(i + 1)
-                if i == -1:
+                if i == 0:
+                    w_int(0)
                     il_p()
-                mm1(i - 1)
+                mm1(i)
                 mm0(i - 1)
-                do_tg(i + 2, TG_ON_G and i >= 0)
+                do_tg(i + 2, i >= 0)
                 prod(i, 0, 0)
                 prod(i, 0, 1)
                 prod(i, 1, 0)
@@ -383,21 +425,26 @@ def tile_capsulenetwork_pb_v_kernel(tc, p, Wr, s, grad_out, out_0, out_1):
                 tt(i + 1, "a", "r", "w")
                 add(i, 1)
                 sm_n1(i + 1)
+                il_s = IL_ON_S and i != 0
+                if il_s:
+                    il(i, 1, True)
                 tr(i)
-                il(i, 0)
+                il(i, 0, False)
                 tt(i + 1, "b", "a", "r")
-                il(i, 1)
+                if not il_s:
+                    il(i, 1, False)
                 sm_nd(i + 1)
                 sm_h(i + 1)
-                quant(i, "ds_int", "dsq", E5)
                 sm_na(i + 1)
-                if i == 0:
-                    quant_p()
                 quant(i, "wi", "wq", E4)
                 sm_c(i + 1)
+                if i == 0:
+                    quant_p()
+                quant_ds(i)
                 quant(i, "dst_in", "dtq", E5)
                 back(i + 1)
-                w_int(i + 1)
+                if i >= 0:
+                    w_int(i + 1)
             for t in range(4):
                 if t < 2:
                     nc.scalar.activation(out=o0[:, t, :], in_=acc[t][:], func=ACT.Copy, scale=INV_K)

@@ -54,6 +54,8 @@ def tile_capsulenetwork_pb_v_kernel(tc, p, Wr, s, grad_out, out_0, out_1):
         nc.vector.memset(eps_t[:], EPS)
         one_t = const.tile([P, 1], F32, name="one_t", tag="one_t")
         nc.vector.memset(one_t[:], 1.0)
+        mhalf_t = const.tile([P, 1], F32, name="mhalf_t", tag="mhalf_t")
+        nc.vector.memset(mhalf_t[:], -0.5)
         warm = const.tile([P, 1], F32, name="warm", tag="warm")
         nc.scalar.activation(out=warm[:], in_=one_t[:], func=ACT.Abs_reciprocal_sqrt)
 
@@ -120,65 +122,48 @@ def tile_capsulenetwork_pb_v_kernel(tc, p, Wr, s, grad_out, out_0, out_1):
             if k == 0:
                 for hh in range(2):
                     nc.scalar.activation(
-                        out=sq[:, :, 64 * hh:64 * hh + 64].rearrange("q (a b) c -> q a c b", a=4),
-                        in_=st[("s", k)][:, 2 * hh:2 * hh + 2, :].rearrange("q t (j a b) -> q a (t j) b", a=4, b=4),
-                        func=ACT.Square,
-                    )
+                        out=omajor(sq, 64 * hh, 64 * hh + 64), in_=by_o(st[("s", k)], 2 * hh, 2 * hh + 2),
+                        func=ACT.Square)
             else:
-                nc.scalar.activation(
-                    out=sq[:].rearrange("q (a b) c -> q a c b", a=4),
-                    in_=st[("s", k)][:].rearrange("q t (j a b) -> q a (t j) b", a=4, b=4),
-                    func=ACT.Square,
-                )
+                nc.scalar.activation(out=omajor(sq, 0, P), in_=by_o(st[("s", k)], 0, 4), func=ACT.Square)
             st[("sq", k)] = sq
+
+        def omajor(tile_ap, c_lo, c_hi):
+            return tile_ap[:, :, c_lo:c_hi].rearrange("q (a b) c -> q a c b", a=4)
+
+        def by_o(tile_ap, t_lo, t_hi):
+            return tile_ap[:, t_lo:t_hi, :].rearrange("q t (j a b) -> q a (t j) b", a=4, b=4)
 
         def do_tg(k, on_g):
             if not ok(k):
                 return
-            tg = big.tile([P, 4, CW], F32, name="tg", tag="tg", bufs=2)
+            tg = big.tile([P, 16, P], F32, name="tg", tag="tg", bufs=2)
             st[("tg", k)] = tg
             if on_g:
                 nc.vector.memset(tg[:, 0, 0:1], 0.0)
-                nc.gpsimd.tensor_tensor(out=tg[:], in0=st[("s", k)][:], in1=st[("g", k)][:], op=ALU.mult)
+                nc.gpsimd.tensor_tensor(
+                    out=omajor(tg, 0, P), in0=by_o(st[("s", k)], 0, 4), in1=by_o(st[("g", k)], 0, 4), op=ALU.mult)
                 return
             for hh in range(2):
-                if True:
-                    out_ap = tg[:].rearrange("q t x -> q (t x)").rearrange("q (o c) -> q o c", o=16)[
-                        :, :, 64 * hh:64 * hh + 64].rearrange("q (a b) c -> q a c b", a=4)
-                    nc.vector.tensor_tensor(
-                        out=out_ap,
-                        in0=st[("s", k)][:, 2 * hh:2 * hh + 2, :].rearrange("q t (j a b) -> q a (t j) b", a=4, b=4),
-                        in1=st[("g", k)][:, 2 * hh:2 * hh + 2, :].rearrange("q t (j a b) -> q a (t j) b", a=4, b=4),
-                        op=ALU.mult,
-                    )
-                else:
-                    nc.vector.tensor_tensor(
-                        out=tg[:, 2 * hh:2 * hh + 2, :],
-                        in0=st[("s", k)][:, 2 * hh:2 * hh + 2, :],
-                        in1=st[("g", k)][:, 2 * hh:2 * hh + 2, :],
-                        op=ALU.mult,
-                    )
+                nc.vector.tensor_tensor(
+                    out=omajor(tg, 64 * hh, 64 * hh + 64),
+                    in0=by_o(st[("s", k)], 2 * hh, 2 * hh + 2),
+                    in1=by_o(st[("g", k)], 2 * hh, 2 * hh + 2),
+                    op=ALU.mult,
+                )
 
         def red(k):
             if not ok(k):
                 return
             qd = psq.tile([P, 2, P], F32, name="qd", tag="qd")
             st[("qd", k)] = qd
-            sq = st[("sq", k)]
-            for o in range(16):
-                nc.tensor.matmul(
-                    out=qd[:, 0, :], lhsT=sq[:, o, :], rhs=ident[:],
-                    is_transpose=True, start=(o == 0), stop=(o == 15),
-                )
-            if k < 2:
-                view = st[("tg", k)][:].rearrange("q t x -> q (t x)").rearrange("q (o c) -> q c o", o=16)
-            else:
-                view = st[("tg", k)][:].rearrange("q t (j o) -> q (t j) o", o=16)
-            for o in range(16):
-                nc.tensor.matmul(
-                    out=qd[:, 1, :], lhsT=view[:, :, o], rhs=ident[:],
-                    is_transpose=True, start=(o == 0), stop=(o == 15),
-                )
+            for w in range(2):
+                src = st[(("sq", "tg")[w], k)]
+                for o in range(16):
+                    nc.tensor.matmul(
+                        out=qd[:, w, :], lhsT=src[:, o, :], rhs=ident[:],
+                        is_transpose=True, start=(o == 0), stop=(o == 15),
+                    )
 
         def smt(k, nm):
             tl = sm.tile([P, P], F32, name=nm, tag=nm)
@@ -191,8 +176,7 @@ def tile_capsulenetwork_pb_v_kernel(tc, p, Wr, s, grad_out, out_0, out_1):
             q = st[("qd", k)][:, 0, :]
             nc.scalar.activation(out=smt(k, "r")[:], in_=q, func=ACT.Abs_reciprocal_sqrt, bias=eps_t[:, 0:1])
             nc.scalar.activation(out=smt(k, "v")[:], in_=q, func=ACT.Abs_reciprocal_sqrt, bias=one_t[:, 0:1])
-            nc.scalar.copy(out=smt(k, "qs")[:], in_=q)
-            nc.scalar.copy(out=smt(k, "dt")[:], in_=st[("qd", k)][:, 1, :])
+            nc.scalar.activation(out=smt(k, "sqh")[:], in_=q, func=ACT.Square, bias=mhalf_t[:, 0:1])
             nc.scalar.activation(out=smt(k, "w")[:], in_=st[("v", k)][:], func=ACT.Square)
 
         def tt(k, nm, x, y):
@@ -200,19 +184,11 @@ def tile_capsulenetwork_pb_v_kernel(tc, p, Wr, s, grad_out, out_0, out_1):
                 return
             nc.vector.tensor_tensor(out=smt(k, nm)[:], in0=st[(x, k)][:], in1=st[(y, k)][:], op=ALU.mult)
 
-        def sm_n1(k):
-            if not ok(k):
-                return
-            nc.vector.scalar_tensor_tensor(
-                out=smt(k, "n1")[:], in0=st[("qs", k)][:], scalar=1.0, in1=st[("qs", k)][:],
-                op0=ALU.subtract, op1=ALU.mult,
-            )
-
         def sm_nd(k):
             if not ok(k):
                 return
             nc.vector.scalar_tensor_tensor(
-                out=smt(k, "nd")[:], in0=st[("n1", k)][:], scalar=2.0 * EPS, in1=st[("dt", k)][:],
+                out=smt(k, "nd")[:], in0=st[("sqh", k)][:], scalar=0.25 + 2.0 * EPS, in1=st[("qd", k)][:, 1, :],
                 op0=ALU.subtract, op1=ALU.mult,
             )
 
@@ -229,7 +205,7 @@ def tile_capsulenetwork_pb_v_kernel(tc, p, Wr, s, grad_out, out_0, out_1):
                 return
             hc = sm.tile([P, 2, P], F32, name="hc", tag="hc")
             st[("hc", k)] = hc
-            nc.vector.tensor_tensor(out=hc[:, 0, :], in0=st[("qs", k)][:], in1=st[("a", k)][:], op=ALU.mult)
+            nc.vector.tensor_tensor(out=hc[:, 0, :], in0=st[("qd", k)][:, 0, :], in1=st[("a", k)][:], op=ALU.mult)
 
         def sm_c(k):
             if not ok(k):
@@ -244,19 +220,17 @@ def tile_capsulenetwork_pb_v_kernel(tc, p, Wr, s, grad_out, out_0, out_1):
                 nc.tensor.transpose(out=hp[:, w, :], in_=st[("hc", k)][:, w, :], identity=ident[:])
             st[("hp", k)] = hp
 
-        def prod(k, w, hh):
+        def prod(k, w):
             if not ok(k):
                 return
             nm = ("pa", "pb")[w]
-            if hh == 0:
-                tl = big.tile([P, 4, CW], F32, name=nm, tag=nm)
-                st[(nm, k)] = tl
-            tl = st[(nm, k)]
+            tl = big.tile([P, 4, CW], F32, name=nm, tag=nm)
+            st[(nm, k)] = tl
             src = st[(("g", "s")[w], k)]
             nc.vector.tensor_tensor(
-                out=tl[:, 2 * hh:2 * hh + 2, :].rearrange("q t (j o) -> q (t j) o", o=16),
-                in0=st[("hp", k)][:, w, 64 * hh:64 * hh + 64].unsqueeze(2).to_broadcast([P, 64, 16]),
-                in1=src[:, 2 * hh:2 * hh + 2, :].rearrange("q t (j o) -> q (t j) o", o=16),
+                out=tl[:].rearrange("q t (j o) -> q (t j) o", o=16),
+                in0=st[("hp", k)][:, w, :].unsqueeze(2).to_broadcast([P, P, 16]),
+                in1=src[:].rearrange("q t (j o) -> q (t j) o", o=16),
                 op=ALU.mult,
             )
 
@@ -417,14 +391,12 @@ def tile_capsulenetwork_pb_v_kernel(tc, p, Wr, s, grad_out, out_0, out_1):
                 mm1(i)
                 mm0(i - 1)
                 do_tg(i + 2, i >= 0)
-                prod(i, 0, 0)
-                prod(i, 0, 1)
-                prod(i, 1, 0)
-                prod(i, 1, 1)
+                prod(i, 0)
+                prod(i, 1)
+                sm_nd(i + 1)
                 add(i, 0)
                 tt(i + 1, "a", "r", "w")
                 add(i, 1)
-                sm_n1(i + 1)
                 il_s = IL_ON_S and i != 0
                 if il_s:
                     il(i, 1, True)
@@ -433,7 +405,6 @@ def tile_capsulenetwork_pb_v_kernel(tc, p, Wr, s, grad_out, out_0, out_1):
                 tt(i + 1, "b", "a", "r")
                 if not il_s:
                     il(i, 1, False)
-                sm_nd(i + 1)
                 sm_h(i + 1)
                 sm_na(i + 1)
                 quant(i, "wi", "wq", E4)

@@ -9,422 +9,390 @@ F32 = mybir.dt.float32
 BF16 = mybir.dt.bfloat16
 U32 = mybir.dt.uint32
 U8 = mybir.dt.uint8
-E4 = mybir.dt.float8_e4m3fn_x4
-E5 = mybir.dt.float8_e5m2_x4
+E4M3 = mybir.dt.float8_e4m3fn_x4
+E5M2 = mybir.dt.float8_e5m2_x4
 ACT = mybir.ActivationFunctionType
 ALU = mybir.AluOpType
-AX = mybir.AxisListType
 
 P = 128
-CW = 512
-NCH = 8
+SLOTS = 4
+CHUNK = 512
+N_CHUNKS = 8
+O = 16
 NI = 512
+N_PRIMARY = 32
+HALF = P // 2
 EPS = 1e-8
-INV_K = 1.0 / 256.0
+COUPLING = 1.0 / 256.0
 
-IL_ON_S = True
-MANUAL = True
 GROUPS = ((0, 1), (2, 3), (4, 5), (6,), (7,))
-MM1_PLAN = {2: ((0, 0, 4),), 3: ((0, 4, 8),), 4: ((1, 0, 4),), 5: ((1, 4, 8),), 6: ((2, 0, 8),), 7: ((3, 0, 4),), 8: ((4, 0, 4),)}
+OUT1_PASSES = {2: ((0, 0, 4),), 3: ((0, 4, 8),), 4: ((1, 0, 4),), 5: ((1, 4, 8),),
+               6: ((2, 0, 8),), 7: ((3, 0, 4),), 8: ((4, 0, 4),)}
+WR_LOADS = {0: (0,), 1: (1,), 2: (2,), 3: (3,), 4: (4, 5), 5: (6, 7)}
 
 
 def tile_capsulenetwork_pb_v_kernel(tc, p, Wr, s, grad_out, out_0, out_1):
     nc = tc.nc
-    s_v = s.rearrange("(p t) j o -> p t (j o)", t=4)
-    g_v = grad_out.rearrange("(p t) j o -> p t (j o)", t=4)
-    w_v = Wr.rearrange("n j o i -> n (j o) i")
-    o1_v = out_1.rearrange("n j o i -> n (j o) i")
+    s_hbm = s.rearrange("(q t) j o -> q t (j o)", t=SLOTS)
+    g_hbm = grad_out.rearrange("(q t) j o -> q t (j o)", t=SLOTS)
+    wr_hbm = Wr.rearrange("n j o i -> n (j o) i")
+    out1_hbm = out_1.rearrange("n j o i -> n (j o) i")
 
     with ExitStack() as ctx:
         const = ctx.enter_context(tc.tile_pool(name="const", bufs=1))
-        ld = ctx.enter_context(tc.tile_pool(name="ld", bufs=4))
-        big = ctx.enter_context(tc.tile_pool(name="big", bufs=1))
-        sm = ctx.enter_context(tc.tile_pool(name="sm", bufs=2))
-        qin = ctx.enter_context(tc.tile_pool(name="qin", bufs=2))
-        cod = ctx.enter_context(tc.tile_pool(name="cod", bufs=2))
-        outp = ctx.enter_context(tc.tile_pool(name="outp", bufs=2))
-        psa = ctx.enter_context(tc.psum_pool(name="psa", bufs=1))
-        psq = ctx.enter_context(tc.psum_pool(name="psq", bufs=1))
-        psh = ctx.enter_context(tc.psum_pool(name="psh", bufs=1))
-        psw = ctx.enter_context(tc.psum_pool(name="psw", bufs=2))
+        loads = ctx.enter_context(tc.tile_pool(name="loads", bufs=4))
+        wide = ctx.enter_context(tc.tile_pool(name="wide", bufs=1))
+        small = ctx.enter_context(tc.tile_pool(name="small", bufs=2))
+        to_quant = ctx.enter_context(tc.tile_pool(name="to_quant", bufs=2))
+        codes = ctx.enter_context(tc.tile_pool(name="codes", bufs=2))
+        stores = ctx.enter_context(tc.tile_pool(name="stores", bufs=2))
+        ps_out0 = ctx.enter_context(tc.psum_pool(name="ps_out0", bufs=1))
+        ps_sums = ctx.enter_context(tc.psum_pool(name="ps_sums", bufs=1))
+        ps_factors = ctx.enter_context(tc.psum_pool(name="ps_factors", bufs=1))
+        ps_turns = ctx.enter_context(tc.psum_pool(name="ps_turns", bufs=2))
 
         ident = const.tile([P, P], F32, name="ident", tag="ident")
         make_identity(nc, ident[:])
-        eps_t = const.tile([P, 1], F32, name="eps_t", tag="eps_t")
-        nc.vector.memset(eps_t[:], EPS)
-        one_t = const.tile([P, 1], F32, name="one_t", tag="one_t")
-        nc.vector.memset(one_t[:], 1.0)
-        mhalf_t = const.tile([P, 1], F32, name="mhalf_t", tag="mhalf_t")
-        nc.vector.memset(mhalf_t[:], -0.5)
-        warm = const.tile([P, 1], F32, name="warm", tag="warm")
-        nc.scalar.activation(out=warm[:], in_=one_t[:], func=ACT.Abs_reciprocal_sqrt)
+        eps_col = const.tile([P, 1], F32, name="eps_col", tag="eps_col")
+        nc.vector.memset(eps_col[:], EPS)
+        one_col = const.tile([P, 1], F32, name="one_col", tag="one_col")
+        nc.vector.memset(one_col[:], 1.0)
+        minus_half_col = const.tile([P, 1], F32, name="minus_half_col", tag="minus_half_col")
+        nc.vector.memset(minus_half_col[:], -0.5)
+        table_warm = const.tile([P, 1], F32, name="table_warm", tag="table_warm")
+        nc.scalar.activation(out=table_warm[:], in_=one_col[:], func=ACT.Abs_reciprocal_sqrt)
 
-        acc = []
-        for t in range(4):
-            acc_t = psa.tile([P, NI], F32, name="acc%d" % t, tag="acc%d" % t)
-            acc.append(acc_t)
+        out0_acc = []
+        for t in range(SLOTS):
+            acc = ps_out0.tile([P, NI], F32, name="out0_acc%d" % t, tag="out0_acc%d" % t)
+            out0_acc.append(acc)
 
         p_codes = const.tile([P, NI], U32, name="p_codes", tag="p_codes", align_bytes=64)
-        p_sc = const.tile([P, NI], U8, name="p_sc", tag="p_sc", align_bytes=64)
-        o0 = const.tile([P, 4, NI], F32, name="o0", tag="o0")
+        p_scales = const.tile([P, NI], U8, name="p_scales", tag="p_scales", align_bytes=64)
+        p_raw = const.tile([P, SLOTS, NI], BF16, name="p_raw", tag="p_raw")
+        p_grouped = const.tile([P, NI, SLOTS], BF16, name="p_grouped", tag="p_grouped", align_bytes=64)
+        out0_sb = const.tile([P, SLOTS, NI], F32, name="out0_sb", tag="out0_sb")
 
-        st = {}
+        live = {}
 
-        def ok(k):
-            return 0 <= k < NCH
+        def is_chunk(k):
+            return 0 <= k < N_CHUNKS
 
-        def load(k):
-            if not ok(k):
+        def group_of(k):
+            grp = [g for g in range(len(GROUPS)) if k in GROUPS[g]][0]
+            return grp, GROUPS[grp].index(k), len(GROUPS[grp])
+
+
+        def load_s_g(k):
+            if not is_chunk(k):
                 return
-            s_t = ld.tile([P, 4, CW], F32, name="s_t", tag="s_t")
-            g_t = ld.tile([P, 4, CW], BF16, name="g_t", tag="g_t")
+            cols = slice(k * CHUNK, (k + 1) * CHUNK)
+            s_t = loads.tile([P, SLOTS, CHUNK], F32, name="s_t", tag="s_t")
+            g_t = loads.tile([P, SLOTS, CHUNK], BF16, name="g_t", tag="g_t")
+            live[("s", k)] = s_t
+            live[("g", k)] = g_t
             if k == 0:
-                for hh in range(2):
-                    nc.sync.dma_start(out=s_t[:, 2 * hh:2 * hh + 2, :], in_=s_v[:, 2 * hh:2 * hh + 2, 0:CW])
-                    nc.sync.dma_start(out=g_t[:, 2 * hh:2 * hh + 2, :], in_=g_v[:, 2 * hh:2 * hh + 2, 0:CW])
+                for half in range(2):
+                    slots = slice(2 * half, 2 * half + 2)
+                    nc.sync.dma_start(out=s_t[:, slots, :], in_=s_hbm[:, slots, cols])
+                    nc.sync.dma_start(out=g_t[:, slots, :], in_=g_hbm[:, slots, cols])
             else:
-                nc.sync.dma_start(out=s_t[:], in_=s_v[:, :, k * CW:(k + 1) * CW])
-                nc.sync.dma_start(out=g_t[:], in_=g_v[:, :, k * CW:(k + 1) * CW])
-            st[("s", k)] = s_t
-            st[("g", k)] = g_t
+                nc.sync.dma_start(out=s_t[:], in_=s_hbm[:, :, cols])
+                nc.sync.dma_start(out=g_t[:], in_=g_hbm[:, :, cols])
 
-        def load_w(k):
-            if not ok(k):
-                return
-            w_raw = ld.tile([P, 32, 64], BF16, name="w_raw", tag="w_raw", bufs=2)
+        def load_wr(k):
+            wr_raw = loads.tile([P, N_PRIMARY, SLOTS * O], BF16, name="wr_raw", tag="wr_raw", bufs=3)
+            live[("wr_raw", k)] = wr_raw
             nc.sync.dma_start(
-                out=w_raw[:],
-                in_=w_v[:, k * CW:(k + 1) * CW, :].rearrange("n (q t) i -> q n (t i)", t=4),
-            )
-            st[("wraw", k)] = w_raw
-
-        def prep_p():
-            p_raw = const.tile([P, 4, NI], BF16, name="p_raw", tag="p_raw")
-            nc.sync.dma_start(out=p_raw[:], in_=p.rearrange("(q t) n i -> q t (n i)", t=4))
-            st["p_raw"] = p_raw
-
-        def il_p():
-            p_int = const.tile([P, NI, 4], BF16, name="p_int", tag="p_int", align_bytes=64)
-            nc.scalar.copy(out=p_int[:], in_=st["p_raw"][:].rearrange("q t c -> q c t"))
-            st["p_int"] = p_int
-
-        def quant_p():
-            p_int = st["p_int"]
-            nc.vector.quantize_mx(
-                out=p_codes[:].bitcast(E4), scales=p_sc[:],
-                in_=p_int[:].rearrange("q c t -> q (c t)"),
+                out=wr_raw[:],
+                in_=wr_hbm[:, k * CHUNK:(k + 1) * CHUNK, :].rearrange("n (m x) i -> m n (x i)", x=SLOTS),
             )
 
-        def do_sq(k):
-            if not ok(k):
+
+        def o_major(tile_ap, col_lo, col_hi):
+            return tile_ap[:, :, col_lo:col_hi].rearrange("q (a b) c -> q a c b", a=4)
+
+        def natural(tile_ap, slot_lo, slot_hi):
+            return tile_ap[:, slot_lo:slot_hi, :].rearrange("q t (j a b) -> q a (t j) b", a=4, b=4)
+
+        def square_s(k):
+            if not is_chunk(k):
                 return
-            sq = big.tile([P, 16, P], F32, name="sq", tag="sq", bufs=2)
+            ss = wide.tile([P, O, P], F32, name="ss", tag="ss", bufs=2)
+            live[("ss", k)] = ss
             if k == 0:
-                for hh in range(2):
+                for half in range(2):
                     nc.scalar.activation(
-                        out=omajor(sq, 64 * hh, 64 * hh + 64), in_=by_o(st[("s", k)], 2 * hh, 2 * hh + 2),
-                        func=ACT.Square)
+                        out=o_major(ss, HALF * half, HALF * (half + 1)),
+                        in_=natural(live[("s", k)], 2 * half, 2 * half + 2), func=ACT.Square)
             else:
-                nc.scalar.activation(out=omajor(sq, 0, P), in_=by_o(st[("s", k)], 0, 4), func=ACT.Square)
-            st[("sq", k)] = sq
+                nc.scalar.activation(out=o_major(ss, 0, P), in_=natural(live[("s", k)], 0, SLOTS), func=ACT.Square)
 
-        def omajor(tile_ap, c_lo, c_hi):
-            return tile_ap[:, :, c_lo:c_hi].rearrange("q (a b) c -> q a c b", a=4)
-
-        def by_o(tile_ap, t_lo, t_hi):
-            return tile_ap[:, t_lo:t_hi, :].rearrange("q t (j a b) -> q a (t j) b", a=4, b=4)
-
-        def do_tg(k, on_g):
-            if not ok(k):
+        def s_times_g(k, on_gpsimd):
+            if not is_chunk(k):
                 return
-            tg = big.tile([P, 16, P], F32, name="tg", tag="tg", bufs=2)
-            st[("tg", k)] = tg
-            if on_g:
-                nc.vector.memset(tg[:, 0, 0:1], 0.0)
+            sg = wide.tile([P, O, P], F32, name="sg", tag="sg", bufs=2)
+            live[("sg", k)] = sg
+            if on_gpsimd:
+                nc.vector.memset(sg[:, 0, 0:1], 0.0)
                 nc.gpsimd.tensor_tensor(
-                    out=omajor(tg, 0, P), in0=by_o(st[("s", k)], 0, 4), in1=by_o(st[("g", k)], 0, 4), op=ALU.mult)
-                return
-            for hh in range(2):
-                nc.vector.tensor_tensor(
-                    out=omajor(tg, 64 * hh, 64 * hh + 64),
-                    in0=by_o(st[("s", k)], 2 * hh, 2 * hh + 2),
-                    in1=by_o(st[("g", k)], 2 * hh, 2 * hh + 2),
-                    op=ALU.mult,
-                )
+                    out=o_major(sg, 0, P), in0=natural(live[("s", k)], 0, SLOTS),
+                    in1=natural(live[("g", k)], 0, SLOTS), op=ALU.mult)
+            else:
+                for half in range(2):
+                    nc.vector.tensor_tensor(
+                        out=o_major(sg, HALF * half, HALF * (half + 1)),
+                        in0=natural(live[("s", k)], 2 * half, 2 * half + 2),
+                        in1=natural(live[("g", k)], 2 * half, 2 * half + 2), op=ALU.mult)
 
-        def red(k):
-            if not ok(k):
+        def capsule_sums(k):
+            if not is_chunk(k):
                 return
-            qd = psq.tile([P, 2, P], F32, name="qd", tag="qd")
-            st[("qd", k)] = qd
-            for w in range(2):
-                src = st[(("sq", "tg")[w], k)]
-                for o in range(16):
+            sums = ps_sums.tile([P, 2, P], F32, name="sums", tag="sums")
+            live[("sums", k)] = sums
+            for which in range(2):
+                products = live[(("ss", "sg")[which], k)]
+                for o in range(O):
                     nc.tensor.matmul(
-                        out=qd[:, w, :], lhsT=src[:, o, :], rhs=ident[:],
-                        is_transpose=True, start=(o == 0), stop=(o == 15),
-                    )
+                        out=sums[:, which, :], lhsT=products[:, o, :], rhs=ident[:],
+                        is_transpose=True, start=(o == 0), stop=(o == O - 1))
 
-        def smt(k, nm):
-            tl = sm.tile([P, P], F32, name=nm, tag=nm)
-            st[(nm, k)] = tl
-            return tl
 
-        def sm_s1(k):
-            if not ok(k):
+        def new_small(k, name):
+            tile_ap = small.tile([P, P], F32, name=name, tag=name)
+            live[(name, k)] = tile_ap
+            return tile_ap
+
+        def factors_on_scalar(k):
+            if not is_chunk(k):
                 return
-            q = st[("qd", k)][:, 0, :]
-            nc.scalar.activation(out=smt(k, "r")[:], in_=q, func=ACT.Abs_reciprocal_sqrt, bias=eps_t[:, 0:1])
-            nc.scalar.activation(out=smt(k, "v")[:], in_=q, func=ACT.Abs_reciprocal_sqrt, bias=one_t[:, 0:1])
-            nc.scalar.activation(out=smt(k, "sqh")[:], in_=q, func=ACT.Square, bias=mhalf_t[:, 0:1])
-            nc.scalar.activation(out=smt(k, "w")[:], in_=st[("v", k)][:], func=ACT.Square)
+            q_sum = live[("sums", k)][:, 0, :]
+            nc.scalar.activation(out=new_small(k, "r")[:], in_=q_sum, func=ACT.Abs_reciprocal_sqrt, bias=eps_col[:, 0:1])
+            nc.scalar.activation(
+                out=new_small(k, "root_w")[:], in_=q_sum, func=ACT.Abs_reciprocal_sqrt, bias=one_col[:, 0:1])
+            nc.scalar.activation(
+                out=new_small(k, "q_shifted_sq")[:], in_=q_sum, func=ACT.Square, bias=minus_half_col[:, 0:1])
+            nc.scalar.activation(out=new_small(k, "w")[:], in_=live[("root_w", k)][:], func=ACT.Square)
 
-        def tt(k, nm, x, y):
-            if not ok(k):
-                return
-            nc.vector.tensor_tensor(out=smt(k, nm)[:], in0=st[(x, k)][:], in1=st[(y, k)][:], op=ALU.mult)
-
-        def sm_nd(k):
-            if not ok(k):
+        def minus_poly_dot(k):
+            if not is_chunk(k):
                 return
             nc.vector.scalar_tensor_tensor(
-                out=smt(k, "nd")[:], in0=st[("sqh", k)][:], scalar=0.25 + 2.0 * EPS, in1=st[("qd", k)][:, 1, :],
-                op0=ALU.subtract, op1=ALU.mult,
-            )
+                out=new_small(k, "minus_poly_dot")[:], in0=live[("q_shifted_sq", k)][:], scalar=0.25 + 2.0 * EPS,
+                in1=live[("sums", k)][:, 1, :], op0=ALU.subtract, op1=ALU.mult)
 
-        def sm_na(k):
-            if not ok(k):
+        def small_product(k, name, left, right):
+            if not is_chunk(k):
                 return
-            nc.vector.scalar_tensor_tensor(
-                out=smt(k, "na")[:], in0=st[("nd", k)][:], scalar=-1.0, in1=st[("a", k)][:],
-                op0=ALU.mult, op1=ALU.mult,
-            )
-
-        def sm_h(k):
-            if not ok(k):
-                return
-            hc = sm.tile([P, 2, P], F32, name="hc", tag="hc")
-            st[("hc", k)] = hc
-            nc.vector.tensor_tensor(out=hc[:, 0, :], in0=st[("qd", k)][:, 0, :], in1=st[("a", k)][:], op=ALU.mult)
-
-        def sm_c(k):
-            if not ok(k):
-                return
-            nc.vector.tensor_tensor(out=st[("hc", k)][:, 1, :], in0=st[("na", k)][:], in1=st[("b", k)][:], op=ALU.mult)
-
-        def back(k):
-            if not ok(k):
-                return
-            hp = psh.tile([P, 2, P], F32, name="hp", tag="hp")
-            for w in range(2):
-                nc.tensor.transpose(out=hp[:, w, :], in_=st[("hc", k)][:, w, :], identity=ident[:])
-            st[("hp", k)] = hp
-
-        def prod(k, w):
-            if not ok(k):
-                return
-            nm = ("pa", "pb")[w]
-            tl = big.tile([P, 4, CW], F32, name=nm, tag=nm)
-            st[(nm, k)] = tl
-            src = st[(("g", "s")[w], k)]
             nc.vector.tensor_tensor(
-                out=tl[:].rearrange("q t (j o) -> q (t j) o", o=16),
-                in0=st[("hp", k)][:, w, :].unsqueeze(2).to_broadcast([P, P, 16]),
-                in1=src[:].rearrange("q t (j o) -> q (t j) o", o=16),
-                op=ALU.mult,
-            )
+                out=new_small(k, name)[:], in0=live[(left, k)][:], in1=live[(right, k)][:], op=ALU.mult)
 
-        def add(k, u):
-            if not ok(k):
+        def factor_h(k):
+            if not is_chunk(k):
+                return
+            h_c = small.tile([P, 2, P], F32, name="h_c", tag="h_c")
+            live[("h_c", k)] = h_c
+            nc.vector.tensor_tensor(out=h_c[:, 0, :], in0=live[("sums", k)][:, 0, :], in1=live[("a", k)][:], op=ALU.mult)
+
+        def poly_dot_a(k):
+            if not is_chunk(k):
+                return
+            nc.vector.scalar_tensor_tensor(
+                out=new_small(k, "poly_dot_a")[:], in0=live[("minus_poly_dot", k)][:], scalar=-1.0,
+                in1=live[("a", k)][:], op0=ALU.mult, op1=ALU.mult)
+
+        def factor_c(k):
+            if not is_chunk(k):
+                return
+            nc.vector.tensor_tensor(
+                out=live[("h_c", k)][:, 1, :], in0=live[("poly_dot_a", k)][:], in1=live[("a_r", k)][:], op=ALU.mult)
+
+        def factors_to_tokens(k):
+            if not is_chunk(k):
+                return
+            factors = ps_factors.tile([P, 2, P], F32, name="factors", tag="factors")
+            live[("factors", k)] = factors
+            for which in range(2):
+                nc.tensor.transpose(out=factors[:, which, :], in_=live[("h_c", k)][:, which, :], identity=ident[:])
+
+
+        def scaled(k, which):
+            if not is_chunk(k):
+                return
+            name = ("h_g", "c_s")[which]
+            product = wide.tile([P, SLOTS, CHUNK], F32, name=name, tag=name)
+            live[(name, k)] = product
+            nc.vector.tensor_tensor(
+                out=product[:].rearrange("q t (j o) -> q (t j) o", o=O),
+                in0=live[("factors", k)][:, which, :].unsqueeze(2).to_broadcast([P, P, O]),
+                in1=live[(("g", "s")[which], k)][:].rearrange("q t (j o) -> q (t j) o", o=O),
+                op=ALU.mult)
+
+        def add_ds(k, u):
+            if not is_chunk(k):
                 return
             if u == 0:
-                ds = qin.tile([P, 4, 2, 256], BF16, name="ds", tag="ds", align_bytes=64)
-                st[("ds", k)] = ds
-            ds = st[("ds", k)]
+                live[("ds", k)] = to_quant.tile([P, SLOTS, 2, CHUNK // 2], BF16, name="ds", tag="ds", align_bytes=64)
             nc.vector.tensor_tensor(
-                out=ds[:, :, u, :].rearrange("q t (m e) -> q t m e", e=2),
-                in0=st[("pa", k)][:].rearrange("q t (m u e) -> q u t m e", u=2, e=2)[:, u],
-                in1=st[("pb", k)][:].rearrange("q t (m u e) -> q u t m e", u=2, e=2)[:, u],
-                op=ALU.add,
-            )
+                out=live[("ds", k)][:, :, u, :].rearrange("q t (m e) -> q t m e", e=2),
+                in0=live[("h_g", k)][:].rearrange("q t (m u e) -> q u t m e", u=2, e=2)[:, u],
+                in1=live[("c_s", k)][:].rearrange("q t (m u e) -> q u t m e", u=2, e=2)[:, u],
+                op=ALU.add)
 
-        def tr(k):
-            if not ok(k):
+        def transpose_ds(k):
+            if not is_chunk(k):
                 return
-            dsw = st[("ds", k)][:].rearrange("q t u x -> q (t u x)").bitcast(F32).rearrange(
-                "q (t u m) -> q t u m", t=4, u=2)
-            dst_in = qin.tile([P, NI, 4], BF16, name="dst_in", tag="dst_in", align_bytes=64)
-            st[("dst_in", k)] = dst_in
-            dww = dst_in[:].rearrange("q c k -> q (c k)").bitcast(F32).rearrange(
-                "q (t m u) -> q t m u", t=4, u=2)
-            for hh in range(2):
-                tp = psw.tile([P, 2, 2, P], F32, name="tp", tag="w")
-                for tt in range(2):
+            ds_words = live[("ds", k)][:].rearrange("q t u x -> q (t u x)").bitcast(F32).rearrange(
+                "q (t u m) -> q t u m", t=SLOTS, u=2)
+            ds_t = to_quant.tile([P, NI, SLOTS], BF16, name="ds_t", tag="ds_t", align_bytes=64)
+            live[("ds_t", k)] = ds_t
+            ds_t_words = ds_t[:].rearrange("m c x -> m (c x)").bitcast(F32).rearrange(
+                "m (t q u) -> m t q u", t=SLOTS, u=2)
+            for half in range(2):
+                turned = ps_turns.tile([P, 2, 2, P], F32, name="turned", tag="turn")
+                for t in range(2):
                     for u in range(2):
-                        nc.tensor.transpose(out=tp[:, tt, u, :], in_=dsw[:, 2 * hh + tt, u, :], identity=ident[:])
-                nc.scalar.copy(out=dww[:, 2 * hh:2 * hh + 2, :, :], in_=tp[:].rearrange("q t u m -> q t m u"))
+                        nc.tensor.transpose(out=turned[:, t, u, :], in_=ds_words[:, 2 * half + t, u, :], identity=ident[:])
+                nc.scalar.copy(
+                    out=ds_t_words[:, 2 * half:2 * half + 2, :, :], in_=turned[:].rearrange("m t u q -> m t q u"))
 
-        def grp_of(k):
-            for gi in range(len(GROUPS)):
-                if k in GROUPS[gi]:
-                    return gi, GROUPS[gi].index(k), len(GROUPS[gi])
-            return None
+        def interleave_ds(k, u, engine):
+            if not is_chunk(k):
+                return
+            grp, place, n_in_group = group_of(k)
+            if ("ds_grouped", grp) not in live:
+                live[("ds_grouped", grp)] = to_quant.tile(
+                    [P, 2 * NI, SLOTS], BF16, name="ds_grouped", tag="ds_grouped", align_bytes=64)
+            columns = live[("ds_grouped", grp)][:, 0:NI * n_in_group, :].rearrange("q (a m) t -> q a m t", m=P)
+            m_width = P // n_in_group
+            for low in range(n_in_group):
+                a_first = 4 * low + 2 * u
+                engine(
+                    out=columns[:, a_first:a_first + 2, m_width * place:m_width * (place + 1), :],
+                    in_=live[("ds", k)][:, :, u, :].rearrange("q t (m l e) -> q l e m t", l=n_in_group, e=2)[:, low])
 
-        def il(k, u, on_s):
-            if not ok(k):
-                return
-            gi, gam, gn = grp_of(k)
-            if ("ds_int", gi) not in st:
-                ds_int = qin.tile([P, 2 * NI, 4], BF16, name="ds_int", tag="ds_int", align_bytes=64)
-                st[("ds_int", gi)] = ds_int
-            ds_int = st[("ds_int", gi)]
-            mw = P // gn
-            for lam in range(gn):
-                a0 = 4 * lam + 2 * u
-                out_ap = ds_int[:, 0:NI * gn, :].rearrange("q (a m) t -> q a m t", m=P)[
-                    :, a0:a0 + 2, mw * gam:mw * (gam + 1), :]
-                in_ap = st[("ds", k)][:, :, u, :].rearrange("q t (m l e) -> q l e m t", l=gn, e=2)[:, lam]
-                if on_s:
-                    nc.scalar.copy(out=out_ap, in_=in_ap)
-                else:
-                    nc.vector.tensor_copy(out=out_ap, in_=in_ap)
 
-        def quant_ds(k):
-            if not ok(k):
+        def quantize_chunk(k, source, name, fmt):
+            if not is_chunk(k):
                 return
-            gi, gam, gn = grp_of(k)
-            if gam != gn - 1:
-                return
-            c_t = cod.tile([P, 2 * NI], U32, name="dsq_c", tag="dsq_c", align_bytes=64)
-            s_t = cod.tile([P, 2 * NI], U8, name="dsq_s", tag="dsq_s", align_bytes=64)
+            code_t = codes.tile([P, NI], U32, name=name + "_codes", tag=name + "_codes", bufs=3, align_bytes=64)
+            scale_t = codes.tile([P, NI], U8, name=name + "_scales", tag=name + "_scales", bufs=3, align_bytes=64)
+            live[(name + "_codes", k)] = code_t
+            live[(name + "_scales", k)] = scale_t
             nc.vector.quantize_mx(
-                out=c_t[:, 0:NI * gn].bitcast(E5), scales=s_t[:, 0:NI * gn],
-                in_=st[("ds_int", gi)][:, 0:NI * gn, :].rearrange("q c t -> q (c t)"),
-            )
-            st[("dsq_c", gi)] = c_t
-            st[("dsq_s", gi)] = s_t
+                out=code_t[:].bitcast(fmt), scales=scale_t[:], in_=live[(source, k)][:].rearrange("q c x -> q (c x)"))
 
-        def quant(k, src, dstn, fmt):
-            if not ok(k):
+        def quantize_group(k):
+            if not is_chunk(k):
                 return
-            c_t = cod.tile([P, NI], U32, name=dstn + "_c", tag=dstn + "_c", align_bytes=64)
-            s_t = cod.tile([P, NI], U8, name=dstn + "_s", tag=dstn + "_s", align_bytes=64)
+            grp, place, n_in_group = group_of(k)
+            if place != n_in_group - 1:
+                return
+            code_t = codes.tile([P, 2 * NI], U32, name="ds_codes", tag="ds_codes", align_bytes=64)
+            scale_t = codes.tile([P, 2 * NI], U8, name="ds_scales", tag="ds_scales", align_bytes=64)
+            live[("ds_codes", grp)] = code_t
+            live[("ds_scales", grp)] = scale_t
+            width = NI * n_in_group
             nc.vector.quantize_mx(
-                out=c_t[:].bitcast(fmt), scales=s_t[:],
-                in_=st[(src, k)][:].rearrange("q c t -> q (c t)"),
-            )
-            st[(dstn + "_c", k)] = c_t
-            st[(dstn + "_s", k)] = s_t
+                out=code_t[:, 0:width].bitcast(E5M2), scales=scale_t[:, 0:width],
+                in_=live[("ds_grouped", grp)][:, 0:width, :].rearrange("q c t -> q (c t)"))
 
-        def w_int(k):
-            if not ok(k):
-                return
-            wi = qin.tile([P, NI, 4], BF16, name="wi", tag="wi", align_bytes=64)
+        def interleave_wr(k):
+            wr_grouped = to_quant.tile([P, NI, SLOTS], BF16, name="wr_grouped", tag="wr_grouped", align_bytes=64)
+            live[("wr_grouped", k)] = wr_grouped
             nc.scalar.copy(
-                out=wi[:].rearrange("q (n i) t -> q n i t", i=16),
-                in_=st[("wraw", k)][:].rearrange("q n (t i) -> q n i t", t=4),
-            )
-            st[("wi", k)] = wi
-            load_w(k + 2)
+                out=wr_grouped[:].rearrange("m (n i) x -> m n i x", i=O),
+                in_=live[("wr_raw", k)][:].rearrange("m n (x i) -> m n i x", x=SLOTS))
 
-        def mm1(step):
-            for gi, a_lo, a_hi in MM1_PLAN.get(step, ()):
-                gn = len(GROUPS[gi])
+
+        def out1_passes(step):
+            for grp, a_lo, a_hi in OUT1_PASSES.get(step, ()):
+                n_a = SLOTS * len(GROUPS[grp])
                 if a_lo == 0:
-                    o1 = outp.tile([P, 32, 8, 16], F32, name="o1", tag="o1")
-                    st[("o1", gi)] = o1
-                o1 = st[("o1", gi)]
+                    live[("out1_sb", grp)] = stores.tile([P, N_PRIMARY, 2 * SLOTS, O], F32, name="out1_sb", tag="out1_sb")
+                out1_sb = live[("out1_sb", grp)]
                 for a in range(a_lo, a_hi):
-                    ot = psw.tile([P, NI], F32, name="ot", tag="w")
+                    prod = ps_turns.tile([P, NI], F32, name="out1_ps", tag="turn")
                     nc.tensor.matmul_mx(
-                        out=ot[:],
-                        lhsT=st[("dsq_c", gi)][:, a * P:(a + 1) * P].bitcast(E5),
-                        lhsT_scale=st[("dsq_s", gi)][:, a * P:(a + 1) * P],
-                        rhs=p_codes[:].bitcast(E4), rhs_scale=p_sc[:],
-                        start=True, stop=True,
-                    )
-                    if gi == len(GROUPS) - 1 and a % 2 == 1:
-                        nc.vector.tensor_scalar_mul(
-                            out=o1[:, :, a, :], in0=ot[:].rearrange("q (n i) -> q n i", i=16), scalar1=INV_K)
+                        out=prod[:],
+                        lhsT=live[("ds_codes", grp)][:, a * P:(a + 1) * P].bitcast(E5M2),
+                        lhsT_scale=live[("ds_scales", grp)][:, a * P:(a + 1) * P],
+                        rhs=p_codes[:].bitcast(E4M3), rhs_scale=p_scales[:], start=True, stop=True)
+                    by_n = prod[:].rearrange("m (n i) -> m n i", i=O)
+                    if grp == len(GROUPS) - 1 and a % 2 == 1:
+                        nc.vector.tensor_scalar_mul(out=out1_sb[:, :, a, :], in0=by_n, scalar1=COUPLING)
                     else:
-                        nc.scalar.activation(
-                            out=o1[:, :, a, :], in_=ot[:].rearrange("q (n i) -> q n i", i=16),
-                            func=ACT.Copy, scale=INV_K,
-                        )
-                if a_hi == 4 * gn:
-                    lo = GROUPS[gi][0] * CW
+                        nc.scalar.activation(out=out1_sb[:, :, a, :], in_=by_n, func=ACT.Copy, scale=COUPLING)
+                if a_hi == n_a:
+                    first = GROUPS[grp][0] * CHUNK
                     nc.scalar.dma_start(
-                        out=o1_v[:, lo:lo + gn * CW, :].rearrange("n (m a) i -> m n (a i)", a=4 * gn),
-                        in_=o1[:, :, 0:4 * gn, :].rearrange("q n a i -> q n (a i)"),
-                    )
+                        out=out1_hbm[:, first:first + P * n_a, :].rearrange("n (m a) i -> m n (a i)", a=n_a),
+                        in_=out1_sb[:, :, 0:n_a, :].rearrange("m n a i -> m n (a i)"))
 
-        def mm0(k):
-            if not ok(k):
+        def out0_pass(k):
+            if not is_chunk(k):
                 return
-            for t in range(4):
+            for t in range(SLOTS):
                 nc.tensor.matmul_mx(
-                    out=acc[t][:],
-                    lhsT=st[("dtq_c", k)][:, t * P:(t + 1) * P].bitcast(E5),
-                    lhsT_scale=st[("dtq_s", k)][:, t * P:(t + 1) * P],
-                    rhs=st[("wq_c", k)][:].bitcast(E4), rhs_scale=st[("wq_s", k)][:],
-                    start=(k == 0), stop=(k == NCH - 1),
-                )
+                    out=out0_acc[t][:],
+                    lhsT=live[("ds_t_codes", k)][:, t * P:(t + 1) * P].bitcast(E5M2),
+                    lhsT_scale=live[("ds_t_scales", k)][:, t * P:(t + 1) * P],
+                    rhs=live[("wr_codes", k)][:].bitcast(E4M3), rhs_scale=live[("wr_scales", k)][:],
+                    start=(k == 0), stop=(k == N_CHUNKS - 1))
 
-        def body():
-            for i in range(-3, NCH + 1):
+        with tc.manual_schedule():
+            for i in range(-3, N_CHUNKS + 1):
                 if i == -3:
-                    load(0)
-                    load(1)
-                    load(2)
-                    load_w(0)
-                    prep_p()
-                    load(3)
-                    load_w(1)
+                    load_s_g(0)
+                    load_s_g(1)
+                    load_s_g(2)
+                    nc.sync.dma_start(out=p_raw[:], in_=p.rearrange("(q t) n i -> q t (n i)", t=SLOTS))
+                    load_s_g(3)
                 elif i > 0:
-                    load(i + 3)
-                do_sq(i + 2)
-                red(i + 1)
-                sm_s1(i + 1)
+                    load_s_g(i + 3)
+                for k in WR_LOADS.get(i, ()):
+                    load_wr(k)
+                square_s(i + 2)
+                capsule_sums(i + 1)
+                factors_on_scalar(i + 1)
                 if i == 0:
-                    w_int(0)
-                    il_p()
-                mm1(i)
-                mm0(i - 1)
-                do_tg(i + 2, i >= 0)
-                prod(i, 0)
-                prod(i, 1)
-                sm_nd(i + 1)
-                add(i, 0)
-                tt(i + 1, "a", "r", "w")
-                add(i, 1)
-                il_s = IL_ON_S and i != 0
-                if il_s:
-                    il(i, 1, True)
-                tr(i)
-                il(i, 0, False)
-                tt(i + 1, "b", "a", "r")
-                if not il_s:
-                    il(i, 1, False)
-                sm_h(i + 1)
-                sm_na(i + 1)
-                quant(i, "wi", "wq", E4)
-                sm_c(i + 1)
+                    nc.scalar.copy(out=p_grouped[:], in_=p_raw[:].rearrange("q t c -> q c t"))
+                out1_passes(i)
+                out0_pass(i - 2)
+                if i == N_CHUNKS:
+                    out0_pass(i - 1)
+                s_times_g(i + 2, i >= 0)
+                scaled(i, 0)
+                scaled(i, 1)
+                minus_poly_dot(i + 1)
+                add_ds(i, 0)
+                small_product(i + 1, "a", "r", "w")
+                add_ds(i, 1)
+                interleave_ds(i, 1, nc.scalar.copy)
+                transpose_ds(i)
+                interleave_ds(i, 0, nc.vector.tensor_copy)
+                small_product(i + 1, "a_r", "a", "r")
+                factor_h(i + 1)
+                poly_dot_a(i + 1)
+                if i < N_CHUNKS:
+                    quantize_chunk(i - 1, "wr_grouped", "wr", E4M3)
+                if i == N_CHUNKS - 1:
+                    quantize_chunk(i, "wr_grouped", "wr", E4M3)
+                factor_c(i + 1)
                 if i == 0:
-                    quant_p()
-                quant_ds(i)
-                quant(i, "dst_in", "dtq", E5)
-                back(i + 1)
-                if i >= 0:
-                    w_int(i + 1)
-            for t in range(4):
-                if t < 2:
-                    nc.scalar.activation(out=o0[:, t, :], in_=acc[t][:], func=ACT.Copy, scale=INV_K)
-                else:
-                    nc.vector.tensor_scalar_mul(out=o0[:, t, :], in0=acc[t][:], scalar1=INV_K)
-            nc.sync.dma_start(out=out_0.rearrange("(q t) n i -> q t (n i)", t=4), in_=o0[:])
+                    nc.vector.quantize_mx(
+                        out=p_codes[:].bitcast(E4M3), scales=p_scales[:], in_=p_grouped[:].rearrange("q c t -> q (c t)"))
+                quantize_group(i)
+                quantize_chunk(i, "ds_t", "ds_t", E5M2)
+                factors_to_tokens(i + 1)
+                if 0 <= i < N_CHUNKS - 1:
+                    interleave_wr(i)
+                if i == N_CHUNKS - 2:
+                    interleave_wr(i + 1)
 
-        if MANUAL:
-            with tc.manual_schedule():
-                body()
-        else:
-            body()
+            for t in range(SLOTS):
+                if t < 2:
+                    nc.scalar.activation(out=out0_sb[:, t, :], in_=out0_acc[t][:], func=ACT.Copy, scale=COUPLING)
+                else:
+                    nc.vector.tensor_scalar_mul(out=out0_sb[:, t, :], in0=out0_acc[t][:], scalar1=COUPLING)
+            nc.sync.dma_start(out=out_0.rearrange("(q t) n i -> q t (n i)", t=SLOTS), in_=out0_sb[:])

from contextlib import ExitStack

import concourse.mybir as mybir
from concourse.masks import make_identity

FLOPS = 2 * 2 * 512 * 512 * 4096

F32 = mybir.dt.float32
BF16 = mybir.dt.bfloat16
U32 = mybir.dt.uint32
U8 = mybir.dt.uint8
E4M3 = mybir.dt.float8_e4m3fn_x4
E5M2 = mybir.dt.float8_e5m2_x4
ACT = mybir.ActivationFunctionType
ALU = mybir.AluOpType

P = 128
SLOTS = 4
CHUNK = 512
N_CHUNKS = 8
O = 16
NI = 512
N_PRIMARY = 32
HALF = P // 2
EPS = 1e-8
COUPLING = 1.0 / 256.0

GROUPS = ((0, 1), (2, 3), (4, 5), (6,), (7,))
OUT1_PASSES = {2: ((0, 0, 4),), 3: ((0, 4, 8),), 4: ((1, 0, 4),), 5: ((1, 4, 8),),
               6: ((2, 0, 8),), 7: ((3, 0, 4),), 8: ((4, 0, 4),)}
WR_LOADS = {0: (0,), 1: (1,), 2: (2,), 3: (3,), 4: (4, 5), 5: (6, 7)}


def tile_capsulenetwork_pb_v_kernel(tc, p, Wr, s, grad_out, out_0, out_1):
    nc = tc.nc
    s_hbm = s.rearrange("(q t) j o -> q t (j o)", t=SLOTS)
    g_hbm = grad_out.rearrange("(q t) j o -> q t (j o)", t=SLOTS)
    wr_hbm = Wr.rearrange("n j o i -> n (j o) i")
    out1_hbm = out_1.rearrange("n j o i -> n (j o) i")

    with ExitStack() as ctx:
        const = ctx.enter_context(tc.tile_pool(name="const", bufs=1))
        loads = ctx.enter_context(tc.tile_pool(name="loads", bufs=4))
        wide = ctx.enter_context(tc.tile_pool(name="wide", bufs=1))
        small = ctx.enter_context(tc.tile_pool(name="small", bufs=2))
        to_quant = ctx.enter_context(tc.tile_pool(name="to_quant", bufs=2))
        codes = ctx.enter_context(tc.tile_pool(name="codes", bufs=2))
        stores = ctx.enter_context(tc.tile_pool(name="stores", bufs=2))
        ps_out0 = ctx.enter_context(tc.psum_pool(name="ps_out0", bufs=1))
        ps_sums = ctx.enter_context(tc.psum_pool(name="ps_sums", bufs=1))
        ps_factors = ctx.enter_context(tc.psum_pool(name="ps_factors", bufs=1))
        ps_turns = ctx.enter_context(tc.psum_pool(name="ps_turns", bufs=2))

        ident = const.tile([P, P], F32, name="ident", tag="ident")
        make_identity(nc, ident[:])
        eps_col = const.tile([P, 1], F32, name="eps_col", tag="eps_col")
        nc.vector.memset(eps_col[:], EPS)
        one_col = const.tile([P, 1], F32, name="one_col", tag="one_col")
        nc.vector.memset(one_col[:], 1.0)
        minus_half_col = const.tile([P, 1], F32, name="minus_half_col", tag="minus_half_col")
        nc.vector.memset(minus_half_col[:], -0.5)
        table_warm = const.tile([P, 1], F32, name="table_warm", tag="table_warm")
        nc.scalar.activation(out=table_warm[:], in_=one_col[:], func=ACT.Abs_reciprocal_sqrt)

        out0_acc = []
        for t in range(SLOTS):
            acc = ps_out0.tile([P, NI], F32, name="out0_acc%d" % t, tag="out0_acc%d" % t)
            out0_acc.append(acc)

        p_codes = const.tile([P, NI], U32, name="p_codes", tag="p_codes", align_bytes=64)
        p_scales = const.tile([P, NI], U8, name="p_scales", tag="p_scales", align_bytes=64)
        p_raw = const.tile([P, SLOTS, NI], BF16, name="p_raw", tag="p_raw")
        p_grouped = const.tile([P, NI, SLOTS], BF16, name="p_grouped", tag="p_grouped", align_bytes=64)
        out0_sb = const.tile([P, SLOTS, NI], F32, name="out0_sb", tag="out0_sb")

        live = {}

        def is_chunk(k):
            return 0 <= k < N_CHUNKS

        def group_of(k):
            grp = [g for g in range(len(GROUPS)) if k in GROUPS[g]][0]
            return grp, GROUPS[grp].index(k), len(GROUPS[grp])


        def load_s_g(k):
            if not is_chunk(k):
                return
            cols = slice(k * CHUNK, (k + 1) * CHUNK)
            s_t = loads.tile([P, SLOTS, CHUNK], F32, name="s_t", tag="s_t")
            g_t = loads.tile([P, SLOTS, CHUNK], BF16, name="g_t", tag="g_t")
            live[("s", k)] = s_t
            live[("g", k)] = g_t
            if k == 0:
                for half in range(2):
                    slots = slice(2 * half, 2 * half + 2)
                    nc.sync.dma_start(out=s_t[:, slots, :], in_=s_hbm[:, slots, cols])
                    nc.sync.dma_start(out=g_t[:, slots, :], in_=g_hbm[:, slots, cols])
            else:
                nc.sync.dma_start(out=s_t[:], in_=s_hbm[:, :, cols])
                nc.sync.dma_start(out=g_t[:], in_=g_hbm[:, :, cols])

        def load_wr(k):
            wr_raw = loads.tile([P, N_PRIMARY, SLOTS * O], BF16, name="wr_raw", tag="wr_raw", bufs=3)
            live[("wr_raw", k)] = wr_raw
            nc.sync.dma_start(
                out=wr_raw[:],
                in_=wr_hbm[:, k * CHUNK:(k + 1) * CHUNK, :].rearrange("n (m x) i -> m n (x i)", x=SLOTS),
            )


        def o_major(tile_ap, col_lo, col_hi):
            return tile_ap[:, :, col_lo:col_hi].rearrange("q (a b) c -> q a c b", a=4)

        def natural(tile_ap, slot_lo, slot_hi):
            return tile_ap[:, slot_lo:slot_hi, :].rearrange("q t (j a b) -> q a (t j) b", a=4, b=4)

        def square_s(k):
            if not is_chunk(k):
                return
            ss = wide.tile([P, O, P], F32, name="ss", tag="ss", bufs=2)
            live[("ss", k)] = ss
            if k == 0:
                for half in range(2):
                    nc.scalar.activation(
                        out=o_major(ss, HALF * half, HALF * (half + 1)),
                        in_=natural(live[("s", k)], 2 * half, 2 * half + 2), func=ACT.Square)
            else:
                nc.scalar.activation(out=o_major(ss, 0, P), in_=natural(live[("s", k)], 0, SLOTS), func=ACT.Square)

        def s_times_g(k, on_gpsimd):
            if not is_chunk(k):
                return
            sg = wide.tile([P, O, P], F32, name="sg", tag="sg", bufs=2)
            live[("sg", k)] = sg
            if on_gpsimd:
                nc.vector.memset(sg[:, 0, 0:1], 0.0)
                nc.gpsimd.tensor_tensor(
                    out=o_major(sg, 0, P), in0=natural(live[("s", k)], 0, SLOTS),
                    in1=natural(live[("g", k)], 0, SLOTS), op=ALU.mult)
            else:
                for half in range(2):
                    nc.vector.tensor_tensor(
                        out=o_major(sg, HALF * half, HALF * (half + 1)),
                        in0=natural(live[("s", k)], 2 * half, 2 * half + 2),
                        in1=natural(live[("g", k)], 2 * half, 2 * half + 2), op=ALU.mult)

        def capsule_sums(k):
            if not is_chunk(k):
                return
            sums = ps_sums.tile([P, 2, P], F32, name="sums", tag="sums")
            live[("sums", k)] = sums
            for which in range(2):
                products = live[(("ss", "sg")[which], k)]
                for o in range(O):
                    nc.tensor.matmul(
                        out=sums[:, which, :], lhsT=products[:, o, :], rhs=ident[:],
                        is_transpose=True, start=(o == 0), stop=(o == O - 1))


        def new_small(k, name):
            tile_ap = small.tile([P, P], F32, name=name, tag=name)
            live[(name, k)] = tile_ap
            return tile_ap

        def factors_on_scalar(k):
            if not is_chunk(k):
                return
            q_sum = live[("sums", k)][:, 0, :]
            nc.scalar.activation(out=new_small(k, "r")[:], in_=q_sum, func=ACT.Abs_reciprocal_sqrt, bias=eps_col[:, 0:1])
            nc.scalar.activation(
                out=new_small(k, "root_w")[:], in_=q_sum, func=ACT.Abs_reciprocal_sqrt, bias=one_col[:, 0:1])
            nc.scalar.activation(
                out=new_small(k, "q_shifted_sq")[:], in_=q_sum, func=ACT.Square, bias=minus_half_col[:, 0:1])
            nc.scalar.activation(out=new_small(k, "w")[:], in_=live[("root_w", k)][:], func=ACT.Square)

        def minus_poly_dot(k):
            if not is_chunk(k):
                return
            nc.vector.scalar_tensor_tensor(
                out=new_small(k, "minus_poly_dot")[:], in0=live[("q_shifted_sq", k)][:], scalar=0.25 + 2.0 * EPS,
                in1=live[("sums", k)][:, 1, :], op0=ALU.subtract, op1=ALU.mult)

        def small_product(k, name, left, right):
            if not is_chunk(k):
                return
            nc.vector.tensor_tensor(
                out=new_small(k, name)[:], in0=live[(left, k)][:], in1=live[(right, k)][:], op=ALU.mult)

        def factor_h(k):
            if not is_chunk(k):
                return
            h_c = small.tile([P, 2, P], F32, name="h_c", tag="h_c")
            live[("h_c", k)] = h_c
            nc.vector.tensor_tensor(out=h_c[:, 0, :], in0=live[("sums", k)][:, 0, :], in1=live[("a", k)][:], op=ALU.mult)

        def poly_dot_a(k):
            if not is_chunk(k):
                return
            nc.vector.scalar_tensor_tensor(
                out=new_small(k, "poly_dot_a")[:], in0=live[("minus_poly_dot", k)][:], scalar=-1.0,
                in1=live[("a", k)][:], op0=ALU.mult, op1=ALU.mult)

        def factor_c(k):
            if not is_chunk(k):
                return
            nc.vector.tensor_tensor(
                out=live[("h_c", k)][:, 1, :], in0=live[("poly_dot_a", k)][:], in1=live[("a_r", k)][:], op=ALU.mult)

        def factors_to_tokens(k):
            if not is_chunk(k):
                return
            factors = ps_factors.tile([P, 2, P], F32, name="factors", tag="factors")
            live[("factors", k)] = factors
            for which in range(2):
                nc.tensor.transpose(out=factors[:, which, :], in_=live[("h_c", k)][:, which, :], identity=ident[:])


        def scaled(k, which):
            if not is_chunk(k):
                return
            name = ("h_g", "c_s")[which]
            product = wide.tile([P, SLOTS, CHUNK], F32, name=name, tag=name)
            live[(name, k)] = product
            nc.vector.tensor_tensor(
                out=product[:].rearrange("q t (j o) -> q (t j) o", o=O),
                in0=live[("factors", k)][:, which, :].unsqueeze(2).to_broadcast([P, P, O]),
                in1=live[(("g", "s")[which], k)][:].rearrange("q t (j o) -> q (t j) o", o=O),
                op=ALU.mult)

        def add_ds(k, u):
            if not is_chunk(k):
                return
            if u == 0:
                live[("ds", k)] = to_quant.tile([P, SLOTS, 2, CHUNK // 2], BF16, name="ds", tag="ds", align_bytes=64)
            nc.vector.tensor_tensor(
                out=live[("ds", k)][:, :, u, :].rearrange("q t (m e) -> q t m e", e=2),
                in0=live[("h_g", k)][:].rearrange("q t (m u e) -> q u t m e", u=2, e=2)[:, u],
                in1=live[("c_s", k)][:].rearrange("q t (m u e) -> q u t m e", u=2, e=2)[:, u],
                op=ALU.add)

        def transpose_ds(k):
            if not is_chunk(k):
                return
            ds_words = live[("ds", k)][:].rearrange("q t u x -> q (t u x)").bitcast(F32).rearrange(
                "q (t u m) -> q t u m", t=SLOTS, u=2)
            ds_t = to_quant.tile([P, NI, SLOTS], BF16, name="ds_t", tag="ds_t", align_bytes=64)
            live[("ds_t", k)] = ds_t
            ds_t_words = ds_t[:].rearrange("m c x -> m (c x)").bitcast(F32).rearrange(
                "m (t q u) -> m t q u", t=SLOTS, u=2)
            for half in range(2):
                turned = ps_turns.tile([P, 2, 2, P], F32, name="turned", tag="turn")
                for t in range(2):
                    for u in range(2):
                        nc.tensor.transpose(out=turned[:, t, u, :], in_=ds_words[:, 2 * half + t, u, :], identity=ident[:])
                nc.scalar.copy(
                    out=ds_t_words[:, 2 * half:2 * half + 2, :, :], in_=turned[:].rearrange("m t u q -> m t q u"))

        def interleave_ds(k, u, engine):
            if not is_chunk(k):
                return
            grp, place, n_in_group = group_of(k)
            if ("ds_grouped", grp) not in live:
                live[("ds_grouped", grp)] = to_quant.tile(
                    [P, 2 * NI, SLOTS], BF16, name="ds_grouped", tag="ds_grouped", align_bytes=64)
            columns = live[("ds_grouped", grp)][:, 0:NI * n_in_group, :].rearrange("q (a m) t -> q a m t", m=P)
            m_width = P // n_in_group
            for low in range(n_in_group):
                a_first = 4 * low + 2 * u
                engine(
                    out=columns[:, a_first:a_first + 2, m_width * place:m_width * (place + 1), :],
                    in_=live[("ds", k)][:, :, u, :].rearrange("q t (m l e) -> q l e m t", l=n_in_group, e=2)[:, low])


        def quantize_chunk(k, source, name, fmt):
            if not is_chunk(k):
                return
            code_t = codes.tile([P, NI], U32, name=name + "_codes", tag=name + "_codes", bufs=3, align_bytes=64)
            scale_t = codes.tile([P, NI], U8, name=name + "_scales", tag=name + "_scales", bufs=3, align_bytes=64)
            live[(name + "_codes", k)] = code_t
            live[(name + "_scales", k)] = scale_t
            nc.vector.quantize_mx(
                out=code_t[:].bitcast(fmt), scales=scale_t[:], in_=live[(source, k)][:].rearrange("q c x -> q (c x)"))

        def quantize_group(k):
            if not is_chunk(k):
                return
            grp, place, n_in_group = group_of(k)
            if place != n_in_group - 1:
                return
            code_t = codes.tile([P, 2 * NI], U32, name="ds_codes", tag="ds_codes", align_bytes=64)
            scale_t = codes.tile([P, 2 * NI], U8, name="ds_scales", tag="ds_scales", align_bytes=64)
            live[("ds_codes", grp)] = code_t
            live[("ds_scales", grp)] = scale_t
            width = NI * n_in_group
            nc.vector.quantize_mx(
                out=code_t[:, 0:width].bitcast(E5M2), scales=scale_t[:, 0:width],
                in_=live[("ds_grouped", grp)][:, 0:width, :].rearrange("q c t -> q (c t)"))

        def interleave_wr(k):
            wr_grouped = to_quant.tile([P, NI, SLOTS], BF16, name="wr_grouped", tag="wr_grouped", align_bytes=64)
            live[("wr_grouped", k)] = wr_grouped
            nc.scalar.copy(
                out=wr_grouped[:].rearrange("m (n i) x -> m n i x", i=O),
                in_=live[("wr_raw", k)][:].rearrange("m n (x i) -> m n i x", x=SLOTS))


        def out1_passes(step):
            for grp, a_lo, a_hi in OUT1_PASSES.get(step, ()):
                n_a = SLOTS * len(GROUPS[grp])
                if a_lo == 0:
                    live[("out1_sb", grp)] = stores.tile([P, N_PRIMARY, 2 * SLOTS, O], F32, name="out1_sb", tag="out1_sb")
                out1_sb = live[("out1_sb", grp)]
                for a in range(a_lo, a_hi):
                    prod = ps_turns.tile([P, NI], F32, name="out1_ps", tag="turn")
                    nc.tensor.matmul_mx(
                        out=prod[:],
                        lhsT=live[("ds_codes", grp)][:, a * P:(a + 1) * P].bitcast(E5M2),
                        lhsT_scale=live[("ds_scales", grp)][:, a * P:(a + 1) * P],
                        rhs=p_codes[:].bitcast(E4M3), rhs_scale=p_scales[:], start=True, stop=True)
                    by_n = prod[:].rearrange("m (n i) -> m n i", i=O)
                    if grp == len(GROUPS) - 1 and a % 2 == 1:
                        nc.vector.tensor_scalar_mul(out=out1_sb[:, :, a, :], in0=by_n, scalar1=COUPLING)
                    else:
                        nc.scalar.activation(out=out1_sb[:, :, a, :], in_=by_n, func=ACT.Copy, scale=COUPLING)
                if a_hi == n_a:
                    first = GROUPS[grp][0] * CHUNK
                    nc.scalar.dma_start(
                        out=out1_hbm[:, first:first + P * n_a, :].rearrange("n (m a) i -> m n (a i)", a=n_a),
                        in_=out1_sb[:, :, 0:n_a, :].rearrange("m n a i -> m n (a i)"))

        def out0_pass(k):
            if not is_chunk(k):
                return
            for t in range(SLOTS):
                nc.tensor.matmul_mx(
                    out=out0_acc[t][:],
                    lhsT=live[("ds_t_codes", k)][:, t * P:(t + 1) * P].bitcast(E5M2),
                    lhsT_scale=live[("ds_t_scales", k)][:, t * P:(t + 1) * P],
                    rhs=live[("wr_codes", k)][:].bitcast(E4M3), rhs_scale=live[("wr_scales", k)][:],
                    start=(k == 0), stop=(k == N_CHUNKS - 1))

        with tc.manual_schedule():
            for i in range(-3, N_CHUNKS + 1):
                if i == -3:
                    load_s_g(0)
                    load_s_g(1)
                    load_s_g(2)
                    nc.sync.dma_start(out=p_raw[:], in_=p.rearrange("(q t) n i -> q t (n i)", t=SLOTS))
                    load_s_g(3)
                elif i > 0:
                    load_s_g(i + 3)
                for k in WR_LOADS.get(i, ()):
                    load_wr(k)
                square_s(i + 2)
                capsule_sums(i + 1)
                factors_on_scalar(i + 1)
                if i == 0:
                    nc.scalar.copy(out=p_grouped[:], in_=p_raw[:].rearrange("q t c -> q c t"))
                out1_passes(i)
                out0_pass(i - 2)
                if i == N_CHUNKS:
                    out0_pass(i - 1)
                s_times_g(i + 2, i >= 0)
                scaled(i, 0)
                scaled(i, 1)
                minus_poly_dot(i + 1)
                add_ds(i, 0)
                small_product(i + 1, "a", "r", "w")
                add_ds(i, 1)
                interleave_ds(i, 1, nc.scalar.copy)
                transpose_ds(i)
                interleave_ds(i, 0, nc.vector.tensor_copy)
                small_product(i + 1, "a_r", "a", "r")
                factor_h(i + 1)
                poly_dot_a(i + 1)
                if i < N_CHUNKS:
                    quantize_chunk(i - 1, "wr_grouped", "wr", E4M3)
                if i == N_CHUNKS - 1:
                    quantize_chunk(i, "wr_grouped", "wr", E4M3)
                factor_c(i + 1)
                if i == 0:
                    nc.vector.quantize_mx(
                        out=p_codes[:].bitcast(E4M3), scales=p_scales[:], in_=p_grouped[:].rearrange("q c t -> q (c t)"))
                quantize_group(i)
                quantize_chunk(i, "ds_t", "ds_t", E5M2)
                factors_to_tokens(i + 1)
                if 0 <= i < N_CHUNKS - 1:
                    interleave_wr(i)
                if i == N_CHUNKS - 2:
                    interleave_wr(i + 1)

            for t in range(SLOTS):
                if t < 2:
                    nc.scalar.activation(out=out0_sb[:, t, :], in_=out0_acc[t][:], func=ACT.Copy, scale=COUPLING)
                else:
                    nc.vector.tensor_scalar_mul(out=out0_sb[:, t, :], in0=out0_acc[t][:], scalar1=COUPLING)
            nc.sync.dma_start(out=out_0.rearrange("(q t) n i -> q t (n i)", t=SLOTS), in_=out0_sb[:])
